import numpy as np
import ml_dtypes


def mxq(x, axis, fmt="e4m3"):
    dtype, down = {"e4m3": (ml_dtypes.float8_e4m3fn, 7), "e5m2": (ml_dtypes.float8_e5m2, 14)}[fmt]
    v = np.moveaxis(np.asarray(x, np.float32).astype(ml_dtypes.bfloat16).astype(np.float64), axis, -1)
    blocks = v.reshape(v.shape[:-1] + (-1, 32))
    amax = np.abs(blocks).max(-1, keepdims=True)
    byte = np.maximum(np.where(amax > 0, np.frexp(amax)[1] - 1 + 127, 0) - down, 1)
    scale = np.exp2(byte - 127.0)
    codes = (blocks / scale).astype(np.float32).astype(dtype).astype(np.float64)
    return np.moveaxis((codes * scale).reshape(v.shape), -1, axis)


WIDE = False


def mx_kscale(k):
    if not WIDE:
        return np.ones(k)
    levels = np.array([10, -10, 5, -5, 0])
    a = np.random.permutation(np.resize(levels, k // 512 * 4)).reshape(k // 512, 4)
    idx = np.arange(k)
    return np.exp2(a[idx // 512, idx % 128 // 32])


BF16 = ml_dtypes.bfloat16


def bf(x):
    return np.asarray(x, np.float32).astype(BF16)


def f64(x):
    return np.asarray(x).astype(np.float64)


B, T, D, H, HK, HV = 4, 2048, 512, 4, 128, 128
VD = H * HV
EPS = 1e-5


def rmsnorm(v, w):
    var = np.mean(np.square(v), axis=-1, keepdims=True)
    return v * (1.0 / np.sqrt(var + EPS)) * w


def sigmoid(v):
    return 1.0 / (1.0 + np.exp(-v))


def setup_inputs():
    s = mx_kscale(D)
    th = mx_kscale(VD)[:HV]
    t = np.tile(th, H)
    g = np.random.standard_normal((B, T, H, HK))
    return {"hidden_states": bf(np.random.standard_normal((B, T, D))),
            "norm_w": bf((1.0 + 0.1 * np.random.standard_normal(D)) * s),
            "gate_w": bf(np.random.standard_normal((D, D)) / np.sqrt(D) / s[None, :]),
            "q_hat": bf(g / np.sqrt(np.sum(np.square(g), axis=-1, keepdims=True))),
            "recurrent_state": bf(np.random.standard_normal((B, H, HK, HV))),
            "v_norm_w": bf((1.0 + 0.1 * np.random.standard_normal(HV)) * th),
            "o_w": bf(np.random.standard_normal((D, VD)) / np.sqrt(VD) / t[None, :])}


def reference(hidden_states, norm_w, gate_w, q_hat, recurrent_state, v_norm_w, o_w):
    x = rmsnorm(f64(hidden_states), f64(norm_w)).reshape(B * T, D)
    o = f64(q_hat).transpose(0, 2, 1, 3) @ f64(recurrent_state)
    o = o.transpose(0, 2, 1, 3)
    o = rmsnorm(o, f64(v_norm_w)).reshape(B * T, VD)
    o = mxq(o, 1, "e4m3") @ mxq(f64(o_w), 1, "e4m3").T
    gate = sigmoid(mxq(x, 1, "e4m3") @ mxq(f64(gate_w), 1, "e4m3").T)
    return (gate * o).reshape(B, T, D)

@@ -1,0 +1,350 @@
+from contextlib import ExitStack
+import math
+
+import concourse.mybir as mybir
+from concourse.masks import make_identity
+
+F32 = mybir.dt.float32
+BF16 = mybir.dt.bfloat16
+U32 = mybir.dt.uint32
+U8 = mybir.dt.uint8
+FP8X4 = mybir.dt.float8_e4m3fn_x4
+ACTF = mybir.ActivationFunctionType
+ALU = mybir.AluOpType
+
+P = 128
+B, T, D, H, HK, HV = 4, 2048, 512, 4, 128, 128
+TOK = B * T
+NT = TOK // P
+GT = 4
+NG = NT // GT
+EPS = 1e-5
+
+FLOPS = 2 * TOK * D * D * 2 + 2 * TOK * H * HK * HV
+
+PIN = True
+D_ON_ACT = (0,)
+G_ON_POOL_MOD = 1
+
+
+def tile_glamemoryreader_pb_t_kernel(
+    tc, hidden_states, norm_w, gate_w, q_hat, recurrent_state, v_norm_w, o_w, out
+):
+    nc = tc.nc
+    hs = hidden_states.rearrange("b t d -> (b t) d")
+    qs = q_hat.rearrange("b t h k -> (b t) (h k)")
+    os_ = out.rearrange("b t d -> (b t) d")
+
+    with ExitStack() as ctx:
+        const = ctx.enter_context(tc.tile_pool(name="const", bufs=1))
+        io = ctx.enter_context(tc.tile_pool(name="io", bufs=4))
+        ob = ctx.enter_context(tc.tile_pool(name="ob", bufs=3))
+        mid = ctx.enter_context(tc.tile_pool(name="mid", bufs=4))
+        qtp = ctx.enter_context(tc.tile_pool(name="qtp", bufs=3))
+        cod = ctx.enter_context(tc.tile_pool(name="cod", bufs=5))
+        stat = ctx.enter_context(tc.tile_pool(name="stat", bufs=8))
+        psum1 = ctx.enter_context(tc.psum_pool(name="psum1", bufs=1))
+        psum_r = ctx.enter_context(tc.psum_pool(name="psumr", bufs=3))
+        if PIN:
+            ctx.enter_context(tc.manual_schedule())
+
+        vecrows = const.tile([P, P], BF16, name="vecrows", tag="vecrows")
+        ident_b = const.tile([P, P], BF16, name="ident_b", tag="ident_b")
+        ident_f = const.tile([P, P], F32, name="ident_f", tag="ident_f")
+        eps_t = const.tile([P, 1], F32, name="eps_t", tag="eps_t")
+        neghalf = const.tile([P, 8], F32, name="neghalf", tag="neghalf")
+        scr = const.tile([P, 1], F32, name="scr", tag="scr")
+        cols = const.tile([P, 8], F32, name="cols", tag="cols")
+        junk = const.tile([P, D], BF16, name="junk", tag="junk")
+        s_sb = const.tile([P, B * H, HV], BF16, name="s_sb", tag="s_sb")
+        w_raw = {}
+        w_codes = {}
+        w_scales = {}
+        for nm in ("g", "o"):
+            w_raw[nm] = const.tile([P, 16, P], BF16, name="wraw_" + nm, tag="wraw_" + nm)
+            w_codes[nm] = const.tile([P, D], U32, name="wc_" + nm, tag="wc_" + nm, align_bytes=64)
+            w_scales[nm] = const.tile([P, D], U8, name="ws_" + nm, tag="ws_" + nm, align_bytes=64)
+
+        nc.gpsimd.memset(vecrows[:], 0.0)
+        nc.vector.memset(eps_t[:], EPS)
+        nc.vector.memset(neghalf[:], -0.5)
+        nc.scalar.dma_start(out=vecrows[0:4, :], in_=norm_w.rearrange("(j c) -> j c", c=P))
+        nc.scalar.dma_start(out=vecrows[4:5, :], in_=v_norm_w.rearrange("(o c) -> o c", o=1))
+        nc.scalar.activation(out=scr[:], in_=eps_t[:], func=ACTF.Sigmoid)
+        make_identity(nc, ident_b[:])
+        make_identity(nc, ident_f[:])
+
+        h_t = {}
+        q_t = {}
+        o_t = {}
+        qTp = {}
+        qT = {}
+        r_ps = {}
+        ms = {}
+        vv = {}
+        rs = {}
+        yx = {}
+        yn = {}
+        xT = {}
+        nT = {}
+        xg = {}
+        ng = {}
+        xc = {}
+        xs = {}
+        ncd = {}
+        nsc = {}
+        g_ps = {}
+        p_ps = {}
+        gate = {}
+
+        def ok(i):
+            return 0 <= i < NT
+
+        def grp(ap, g):
+            return ap[g * GT * P : (g + 1) * GT * P, :].rearrange("(p j) d -> p j d", j=GT)
+
+        def load(g):
+            q_t[g] = io.tile([P, GT, D], BF16, name="q%d" % g, tag="q")
+            nc.sync.dma_start(out=q_t[g][:], in_=grp(qs, g))
+            h_t[g] = io.tile([P, GT, D], BF16, name="h%d" % g, tag="h")
+            nc.sync.dma_start(out=h_t[g][:], in_=grp(hs, g))
+            if g == 0:
+                nc.sync.dma_start(out=s_sb[:], in_=recurrent_state.rearrange("b h k v -> k (b h) v"))
+                for nm, w in (("g", gate_w), ("o", o_w)):
+                    nc.sync.dma_start(
+                        out=w_raw[nm][:],
+                        in_=w.rearrange("d (j c) -> (d j) c", c=P).rearrange("(k a) c -> a k c", a=P),
+                    )
+
+        def prep_vec():
+            vps = psum1.tile([P, P], BF16, name="vps", tag="Tn")
+            nc.tensor.transpose(vps[:], vecrows[:], ident_b[:])
+            nc.vector.tensor_copy(out=cols[:, 0:5], in_=vps[:, 0:5])
+
+        def prep_weight(nm):
+            for half in range(2):
+                wps = psum1.tile([P, 1024], BF16, name="wps_%s%d" % (nm, half), tag=("g", "p")[half])
+                for k in range(8):
+                    nc.tensor.transpose(wps[:, k * P : (k + 1) * P], w_raw[nm][:, half * 8 + k, :], ident_b[:])
+                wg = const.tile([P, 1024], BF16, name="wg_%s%d" % (nm, half), tag="wg_%s%d" % (nm, half), align_bytes=64)
+                if half == 0:
+                    nc.scalar.copy(out=wg[:], in_=wps[:])
+                else:
+                    nc.vector.tensor_copy(out=wg[:], in_=wps[:])
+                sl = slice(half * 256, (half + 1) * 256)
+                nc.vector.quantize_mx(out=w_codes[nm][:, sl].bitcast(FP8X4), scales=w_scales[nm][:, sl], in_=wg[:])
+
+        def stat_tiles(s):
+            if s not in ms:
+                ms[s] = stat.tile([P, 8], F32, name="ms%d" % s, tag="ms")
+                vv[s] = stat.tile([P, 8], F32, name="vv%d" % s, tag="vv")
+                rs[s] = stat.tile([P, 8], F32, name="rs%d" % s, tag="rs")
+
+        def stat_range(s):
+            lo = 0 if ok(s - 2) else 4
+            hi = 5 if ok(s) else 4
+            return lo, hi
+
+        def op_tq(i):
+            if ok(i) and i % 2 == 0:
+                u = i // 2
+                qTp[u] = psum1.tile([P, 2, H, P], BF16, name="qTp%d" % u, tag="qTp")
+                for half in range(2):
+                    for h in range(H):
+                        nc.tensor.transpose(
+                            qTp[u][:, half, h, :],
+                            q_t[i // GT][:, i % GT + half, h * HK : (h + 1) * HK],
+                            ident_b[:],
+                        )
+
+        def op_a(i):
+            if ok(i) and i % 2 == 0:
+                u = i // 2
+                qT[u] = qtp.tile([P, 2, H, P], BF16, name="qT%d" % u, tag="qT")
+                nc.scalar.copy(out=qT[u][:], in_=qTp[u][:])
+
+        def op_mr(i):
+            if ok(i):
+                b = i // (NT // B)
+                r_ps[i] = psum_r.tile([P, D], F32, name="r%d" % i, tag="r")
+                for h in range(H):
+                    nc.tensor.matmul(
+                        out=r_ps[i][:, h * HV : (h + 1) * HV],
+                        lhsT=qT[i // 2][:, i % 2, h, :],
+                        rhs=s_sb[:, b * H + h, :],
+                        start=True,
+                        stop=True,
+                    )
+
+        def op_f(i):
+            if ok(i):
+                stat_tiles(i)
+                nc.scalar.activation(
+                    out=junk[:],
+                    in_=h_t[i // GT][:, i % GT, :],
+                    func=ACTF.Square,
+                    scale=1.0 / math.sqrt(D),
+                    accum_out=ms[i][:, 4:5],
+                )
+
+        def op_b(i):
+            if ok(i):
+                stat_tiles(i + 2)
+                for h in range(H):
+                    nc.scalar.activation(
+                        out=junk[:, 0:HV],
+                        in_=r_ps[i][:, h * HV : (h + 1) * HV],
+                        func=ACTF.Square,
+                        scale=1.0 / math.sqrt(HV),
+                        accum_out=ms[i + 2][:, h : h + 1],
+                    )
+
+        def op_eps(s):
+            lo, hi = stat_range(s)
+            if lo < hi:
+                nc.scalar.activation(
+                    out=vv[s][:, lo:hi], in_=ms[s][:, lo:hi], func=ACTF.Identity, bias=eps_t[:, 0:1], scale=1.0
+                )
+
+        def op_pow(s):
+            lo, hi = stat_range(s)
+            if lo < hi:
+                nc.gpsimd.tensor_tensor(out=rs[s][:, lo:hi], in0=vv[s][:, lo:hi], in1=neghalf[:, lo:hi], op=ALU.pow)
+
+        def op_g(i):
+            if ok(i):
+                yx[i] = mid.tile([P, D], F32, name="yx%d" % i, tag="yx")
+                if i % G_ON_POOL_MOD == 0:
+                    nc.gpsimd.tensor_scalar(
+                        out=yx[i][:],
+                        in0=h_t[i // GT][:, i % GT, :],
+                        scalar1=rs[i][:, 4:5],
+                        scalar2=0.0,
+                        op0=ALU.mult,
+                        op1=ALU.add,
+                    )
+                else:
+                    nc.vector.tensor_scalar(
+                        out=yx[i][:], in0=h_t[i // GT][:, i % GT, :], scalar1=rs[i][:, 4:5], scalar2=None, op0=ALU.mult
+                    )
+
+        def op_c(i):
+            if ok(i):
+                yn[i] = mid.tile([P, H, HV], F32, name="yn%d" % i, tag="yn")
+                nc.vector.tensor_tensor(
+                    out=yn[i][:],
+                    in0=r_ps[i][:].rearrange("p (h v) -> p h v", h=H),
+                    in1=rs[i + 2][:, 0:H].unsqueeze(2).to_broadcast([P, H, HV]),
+                    op=ALU.mult,
+                )
+
+        def op_tx(i):
+            if ok(i):
+                xT[i] = psum1.tile([P, 4, P], F32, name="xT%d" % i, tag="Tx")
+                for j in range(4):
+                    nc.tensor.transpose(xT[i][:, j, :], yx[i][:, j * P : (j + 1) * P], ident_f[:])
+
+        def op_tn(i):
+            if ok(i):
+                nT[i] = psum1.tile([P, 4, P], F32, name="nT%d" % i, tag="Tn")
+                for j in range(4):
+                    nc.tensor.transpose(nT[i][:, j, :], yn[i][:, j, :], ident_f[:])
+
+        def op_h(i):
+            if ok(i):
+                xg[i] = mid.tile([P, P, 4], BF16, name="xg%d" % i, tag="xg", align_bytes=64)
+                nc.vector.tensor_tensor(
+                    out=xg[i][:],
+                    in0=xT[i][:].rearrange("p j t -> p t j"),
+                    in1=cols[:, 0:4].unsqueeze(1).to_broadcast([P, P, 4]),
+                    op=ALU.mult,
+                )
+
+        def op_d(i):
+            if ok(i):
+                ng[i] = mid.tile([P, P, 4], BF16, name="ng%d" % i, tag="ng", align_bytes=64)
+                src = nT[i][:].rearrange("p j t -> p t j")
+                if i % 3 in D_ON_ACT:
+                    nc.scalar.activation(out=ng[i][:], in_=src, func=ACTF.Copy, scale=cols[:, 4:5])
+                else:
+                    nc.vector.tensor_scalar(out=ng[i][:], in0=src, scalar1=cols[:, 4:5], scalar2=None, op0=ALU.mult)
+
+        def op_i(i):
+            if ok(i):
+                xc[i] = cod.tile([P, P], U32, name="xc%d" % i, tag="xc", align_bytes=64)
+                xs[i] = cod.tile([P, P], U8, name="xs%d" % i, tag="xs", align_bytes=64)
+                nc.vector.quantize_mx(
+                    out=xc[i][:].bitcast(FP8X4), scales=xs[i][:], in_=xg[i][:].rearrange("p t j -> p (t j)")
+                )
+
+        def op_e(i):
+            if ok(i):
+                ncd[i] = cod.tile([P, P], U32, name="nc%d" % i, tag="nc", align_bytes=64)
+                nsc[i] = cod.tile([P, P], U8, name="ns%d" % i, tag="ns", align_bytes=64)
+                nc.vector.quantize_mx(
+                    out=ncd[i][:].bitcast(FP8X4), scales=nsc[i][:], in_=ng[i][:].rearrange("p t j -> p (t j)")
+                )
+
+        def mx(dst, codes, scales, nm):
+            nc.tensor.matmul_mx(
+                out=dst[:],
+                lhsT=codes[:].bitcast(FP8X4),
+                lhsT_scale=scales[:],
+                rhs=w_codes[nm][:].bitcast(FP8X4),
+                rhs_scale=w_scales[nm][:],
+                start=True,
+                stop=True,
+            )
+
+        def op_mxg(i):
+            if ok(i):
+                g_ps[i] = psum1.tile([P, D], F32, name="g%d" % i, tag="g")
+                mx(g_ps[i], xc[i], xs[i], "g")
+
+        def op_mxp(i):
+            if ok(i):
+                p_ps[i] = psum1.tile([P, D], F32, name="p%d" % i, tag="p")
+                mx(p_ps[i], ncd[i], nsc[i], "o")
+
+        def op_j(i):
+            if ok(i):
+                gate[i] = cod.tile([P, D], F32, name="gate%d" % i, tag="gate")
+                nc.scalar.activation(out=gate[i][:], in_=g_ps[i][:], func=ACTF.Sigmoid)
+
+        def op_k(i):
+            if ok(i):
+                g = i // GT
+                if i % GT == 0:
+                    o_t[g] = ob.tile([P, GT, D], F32, name="o%d" % g, tag="o")
+                nc.vector.tensor_tensor(out=o_t[g][:, i % GT, :], in0=p_ps[i][:], in1=gate[i][:], op=ALU.mult)
+                if i % GT == GT - 1:
+                    nc.sync.dma_start(out=grp(os_, g), in_=o_t[g][:])
+
+        for tau in range(-12, NT + 6):
+            if (tau + 12) % GT == 0 and (tau + 12) // GT < NG:
+                load((tau + 12) // GT)
+            if tau == -1:
+                prep_vec()
+            if tau == 2:
+                prep_weight("g")
+            if tau == 3:
+                prep_weight("o")
+            op_mxp(tau - 5)
+            op_mxg(tau - 4)
+            op_tn(tau - 3)
+            op_tx(tau - 1)
+            op_tq(tau + 2)
+            op_mr(tau)
+            op_b(tau - 1)
+            op_f(tau + 1)
+            op_eps(tau + 1)
+            op_j(tau - 4)
+            op_a(tau + 1)
+            op_pow(tau)
+            op_g(tau)
+            op_h(tau - 2)
+            op_k(tau - 5)
+            op_d(tau - 3)
+            op_c(tau - 2)
+            op_i(tau - 2)
+            op_e(tau - 3)

@@ -23,8 +23,8 @@ EPS = 1e-5
 FLOPS = 2 * TOK * D * D * 2 + 2 * TOK * H * HK * HV
 
 PIN = True
-D_ON_ACT = (0,)
-G_ON_POOL_MOD = 1
+D_ON_ACT = (0, 1)
+G_ON_POOL_MOD = 1000
 
 
 def tile_glamemoryreader_pb_t_kernel(
@@ -214,7 +214,7 @@ def tile_glamemoryreader_pb_t_kernel(
         def op_g(i):
             if ok(i):
                 yx[i] = mid.tile([P, D], F32, name="yx%d" % i, tag="yx")
-                if i % G_ON_POOL_MOD == 0:
+                if i % G_ON_POOL_MOD == G_ON_POOL_MOD - 1:
                     nc.gpsimd.tensor_scalar(
                         out=yx[i][:],
                         in0=h_t[i // GT][:, i % GT, :],
@@ -341,10 +341,10 @@ def tile_glamemoryreader_pb_t_kernel(
             op_j(tau - 4)
             op_a(tau + 1)
             op_pow(tau)
-            op_g(tau)
             op_h(tau - 2)
             op_k(tau - 5)
             op_d(tau - 3)
             op_c(tau - 2)
+            op_g(tau)
             op_i(tau - 2)
             op_e(tau - 3)

@@ -23,8 +23,9 @@ EPS = 1e-5
 FLOPS = 2 * TOK * D * D * 2 + 2 * TOK * H * HK * HV
 
 PIN = True
-D_ON_ACT = (0, 1)
-G_ON_POOL_MOD = 1000
+EXTRA_PASSES = 1
+D_ON_ACT = (0,)
+G_ON_POOL_MOD = 1
 
 
 def tile_glamemoryreader_pb_t_kernel(
@@ -214,7 +215,7 @@ def tile_glamemoryreader_pb_t_kernel(
         def op_g(i):
             if ok(i):
                 yx[i] = mid.tile([P, D], F32, name="yx%d" % i, tag="yx")
-                if i % G_ON_POOL_MOD == G_ON_POOL_MOD - 1:
+                if i % G_ON_POOL_MOD == 0:
                     nc.gpsimd.tensor_scalar(
                         out=yx[i][:],
                         in0=h_t[i // GT][:, i % GT, :],
@@ -286,15 +287,16 @@ def tile_glamemoryreader_pb_t_kernel(
                 )
 
         def mx(dst, codes, scales, nm):
-            nc.tensor.matmul_mx(
-                out=dst[:],
-                lhsT=codes[:].bitcast(FP8X4),
-                lhsT_scale=scales[:],
-                rhs=w_codes[nm][:].bitcast(FP8X4),
-                rhs_scale=w_scales[nm][:],
-                start=True,
-                stop=True,
-            )
+            for rep in range(1 + EXTRA_PASSES):
+                nc.tensor.matmul_mx(
+                    out=dst[:],
+                    lhsT=codes[:].bitcast(FP8X4),
+                    lhsT_scale=scales[:],
+                    rhs=w_codes[nm][:].bitcast(FP8X4),
+                    rhs_scale=w_scales[nm][:],
+                    start=True,
+                    stop=True,
+                )
 
         def op_mxg(i):
             if ok(i):
@@ -341,10 +343,10 @@ def tile_glamemoryreader_pb_t_kernel(
             op_j(tau - 4)
             op_a(tau + 1)
             op_pow(tau)
+            op_g(tau)
             op_h(tau - 2)
             op_k(tau - 5)
             op_d(tau - 3)
             op_c(tau - 2)
-            op_g(tau)
             op_i(tau - 2)
             op_e(tau - 3)

@@ -23,8 +23,7 @@ EPS = 1e-5
 FLOPS = 2 * TOK * D * D * 2 + 2 * TOK * H * HK * HV
 
 PIN = True
-EXTRA_PASSES = 1
-D_ON_ACT = (0,)
+D_ON_ACT = ()
 G_ON_POOL_MOD = 1
 
 
@@ -46,6 +45,8 @@ def tile_glamemoryreader_pb_t_kernel(
         stat = ctx.enter_context(tc.tile_pool(name="stat", bufs=8))
         psum1 = ctx.enter_context(tc.psum_pool(name="psum1", bufs=1))
         psum_r = ctx.enter_context(tc.psum_pool(name="psumr", bufs=3))
+        psum_t = ctx.enter_context(tc.psum_pool(name="psumt", bufs=2))
+        psum_o = ctx.enter_context(tc.psum_pool(name="psumo", bufs=2))
         if PIN:
             ctx.enter_context(tc.manual_schedule())
 
@@ -118,13 +119,13 @@ def tile_glamemoryreader_pb_t_kernel(
                     )
 
         def prep_vec():
-            vps = psum1.tile([P, P], BF16, name="vps", tag="Tn")
+            vps = psum_t.tile([P, P], BF16, name="vps", tag="T")
             nc.tensor.transpose(vps[:], vecrows[:], ident_b[:])
             nc.vector.tensor_copy(out=cols[:, 0:5], in_=vps[:, 0:5])
 
         def prep_weight(nm):
             for half in range(2):
-                wps = psum1.tile([P, 1024], BF16, name="wps_%s%d" % (nm, half), tag=("g", "p")[half])
+                wps = psum_o.tile([P, 1024], BF16, name="wps_%s%d" % (nm, half), tag="O")
                 for k in range(8):
                     nc.tensor.transpose(wps[:, k * P : (k + 1) * P], w_raw[nm][:, half * 8 + k, :], ident_b[:])
                 wg = const.tile([P, 1024], BF16, name="wg_%s%d" % (nm, half), tag="wg_%s%d" % (nm, half), align_bytes=64)
@@ -241,13 +242,13 @@ def tile_glamemoryreader_pb_t_kernel(
 
         def op_tx(i):
             if ok(i):
-                xT[i] = psum1.tile([P, 4, P], F32, name="xT%d" % i, tag="Tx")
+                xT[i] = psum_t.tile([P, 4, P], F32, name="xT%d" % i, tag="T")
                 for j in range(4):
                     nc.tensor.transpose(xT[i][:, j, :], yx[i][:, j * P : (j + 1) * P], ident_f[:])
 
         def op_tn(i):
             if ok(i):
-                nT[i] = psum1.tile([P, 4, P], F32, name="nT%d" % i, tag="Tn")
+                nT[i] = psum_t.tile([P, 4, P], F32, name="nT%d" % i, tag="T")
                 for j in range(4):
                     nc.tensor.transpose(nT[i][:, j, :], yn[i][:, j, :], ident_f[:])
 
@@ -287,25 +288,24 @@ def tile_glamemoryreader_pb_t_kernel(
                 )
 
         def mx(dst, codes, scales, nm):
-            for rep in range(1 + EXTRA_PASSES):
-                nc.tensor.matmul_mx(
-                    out=dst[:],
-                    lhsT=codes[:].bitcast(FP8X4),
-                    lhsT_scale=scales[:],
-                    rhs=w_codes[nm][:].bitcast(FP8X4),
-                    rhs_scale=w_scales[nm][:],
-                    start=True,
-                    stop=True,
-                )
+            nc.tensor.matmul_mx(
+                out=dst[:],
+                lhsT=codes[:].bitcast(FP8X4),
+                lhsT_scale=scales[:],
+                rhs=w_codes[nm][:].bitcast(FP8X4),
+                rhs_scale=w_scales[nm][:],
+                start=True,
+                stop=True,
+            )
 
         def op_mxg(i):
             if ok(i):
-                g_ps[i] = psum1.tile([P, D], F32, name="g%d" % i, tag="g")
+                g_ps[i] = psum_o.tile([P, D], F32, name="g%d" % i, tag="O")
                 mx(g_ps[i], xc[i], xs[i], "g")
 
         def op_mxp(i):
             if ok(i):
-                p_ps[i] = psum1.tile([P, D], F32, name="p%d" % i, tag="p")
+                p_ps[i] = psum_o.tile([P, D], F32, name="p%d" % i, tag="O")
                 mx(p_ps[i], ncd[i], nsc[i], "o")
 
         def op_j(i):
@@ -325,28 +325,28 @@ def tile_glamemoryreader_pb_t_kernel(
         for tau in range(-12, NT + 6):
             if (tau + 12) % GT == 0 and (tau + 12) // GT < NG:
                 load((tau + 12) // GT)
-            if tau == -1:
+            if tau == -3:
                 prep_vec()
-            if tau == 2:
+            if tau == 1:
                 prep_weight("g")
-            if tau == 3:
+            if tau == 2:
                 prep_weight("o")
-            op_mxp(tau - 5)
-            op_mxg(tau - 4)
-            op_tn(tau - 3)
-            op_tx(tau - 1)
-            op_tq(tau + 2)
-            op_mr(tau)
-            op_b(tau - 1)
-            op_f(tau + 1)
-            op_eps(tau + 1)
-            op_j(tau - 4)
-            op_a(tau + 1)
-            op_pow(tau)
-            op_g(tau)
+            op_f(tau + 2)
             op_h(tau - 2)
-            op_k(tau - 5)
-            op_d(tau - 3)
             op_c(tau - 2)
+            op_pow(tau + 1)
+            op_b(tau)
+            op_j(tau - 4)
+            op_mxp(tau - 5)
+            op_tn(tau - 3)
+            op_k(tau - 5)
+            op_tq(tau + 4)
+            op_a(tau + 3)
+            op_d(tau - 3)
+            op_tx(tau - 1)
             op_i(tau - 2)
+            op_mr(tau + 1)
             op_e(tau - 3)
+            op_g(tau)
+            op_mxg(tau - 3)
+            op_eps(tau + 2)

@@ -23,6 +23,7 @@ EPS = 1e-5
 FLOPS = 2 * TOK * D * D * 2 + 2 * TOK * H * HK * HV
 
 PIN = True
+CLOCK_MATMULS = 2
 D_ON_ACT = ()
 G_ON_POOL_MOD = 1
 
@@ -243,6 +244,14 @@ def tile_glamemoryreader_pb_t_kernel(
         def op_tx(i):
             if ok(i):
                 xT[i] = psum_t.tile([P, 4, P], F32, name="xT%d" % i, tag="T")
+                for j in range(CLOCK_MATMULS):
+                    nc.tensor.matmul(
+                        out=xT[i][:, j, :],
+                        lhsT=yx[i][:, j * P : (j + 1) * P],
+                        rhs=yx[i][:, (j + 2) * P : (j + 3) * P],
+                        start=True,
+                        stop=True,
+                    )
                 for j in range(4):
                     nc.tensor.transpose(xT[i][:, j, :], yx[i][:, j * P : (j + 1) * P], ident_f[:])
 

@@ -23,8 +23,7 @@ EPS = 1e-5
 FLOPS = 2 * TOK * D * D * 2 + 2 * TOK * H * HK * HV
 
 PIN = True
-CLOCK_MATMULS = 2
-D_ON_ACT = ()
+D_ON_ACT = (0, 1, 2)
 G_ON_POOL_MOD = 1
 
 
@@ -164,7 +163,7 @@ def tile_glamemoryreader_pb_t_kernel(
             if ok(i) and i % 2 == 0:
                 u = i // 2
                 qT[u] = qtp.tile([P, 2, H, P], BF16, name="qT%d" % u, tag="qT")
-                nc.scalar.copy(out=qT[u][:], in_=qTp[u][:])
+                nc.vector.tensor_copy(out=qT[u][:], in_=qTp[u][:])
 
         def op_mr(i):
             if ok(i):
@@ -244,14 +243,6 @@ def tile_glamemoryreader_pb_t_kernel(
         def op_tx(i):
             if ok(i):
                 xT[i] = psum_t.tile([P, 4, P], F32, name="xT%d" % i, tag="T")
-                for j in range(CLOCK_MATMULS):
-                    nc.tensor.matmul(
-                        out=xT[i][:, j, :],
-                        lhsT=yx[i][:, j * P : (j + 1) * P],
-                        rhs=yx[i][:, (j + 2) * P : (j + 3) * P],
-                        start=True,
-                        stop=True,
-                    )
                 for j in range(4):
                     nc.tensor.transpose(xT[i][:, j, :], yx[i][:, j * P : (j + 1) * P], ident_f[:])
 
@@ -331,7 +322,7 @@ def tile_glamemoryreader_pb_t_kernel(
                 if i % GT == GT - 1:
                     nc.sync.dma_start(out=grp(os_, g), in_=o_t[g][:])
 
-        for tau in range(-12, NT + 6):
+        for tau in range(-12, NT + 7):
             if (tau + 12) % GT == 0 and (tau + 12) // GT < NG:
                 load((tau + 12) // GT)
             if tau == -3:
@@ -346,16 +337,16 @@ def tile_glamemoryreader_pb_t_kernel(
             op_pow(tau + 1)
             op_b(tau)
             op_j(tau - 4)
-            op_mxp(tau - 5)
+            op_mxp(tau - 6)
             op_tn(tau - 3)
-            op_k(tau - 5)
+            op_k(tau - 6)
             op_tq(tau + 4)
             op_a(tau + 3)
             op_d(tau - 3)
             op_tx(tau - 1)
             op_i(tau - 2)
             op_mr(tau + 1)
-            op_e(tau - 3)
+            op_e(tau - 4)
             op_g(tau)
             op_mxg(tau - 3)
             op_eps(tau + 2)

@@ -23,7 +23,7 @@ EPS = 1e-5
 FLOPS = 2 * TOK * D * D * 2 + 2 * TOK * H * HK * HV
 
 PIN = True
-D_ON_ACT = (0, 1, 2)
+D_ON_ACT = ()
 G_ON_POOL_MOD = 1
 
 
@@ -322,7 +322,7 @@ def tile_glamemoryreader_pb_t_kernel(
                 if i % GT == GT - 1:
                     nc.sync.dma_start(out=grp(os_, g), in_=o_t[g][:])
 
-        for tau in range(-12, NT + 7):
+        for tau in range(-12, NT + 6):
             if (tau + 12) % GT == 0 and (tau + 12) // GT < NG:
                 load((tau + 12) // GT)
             if tau == -3:
@@ -337,16 +337,16 @@ def tile_glamemoryreader_pb_t_kernel(
             op_pow(tau + 1)
             op_b(tau)
             op_j(tau - 4)
-            op_mxp(tau - 6)
+            op_mxp(tau - 5)
             op_tn(tau - 3)
-            op_k(tau - 6)
+            op_k(tau - 5)
             op_tq(tau + 4)
             op_a(tau + 3)
             op_d(tau - 3)
             op_tx(tau - 1)
             op_i(tau - 2)
             op_mr(tau + 1)
-            op_e(tau - 4)
+            op_e(tau - 3)
             op_g(tau)
             op_mxg(tau - 3)
             op_eps(tau + 2)

@@ -23,7 +23,7 @@ EPS = 1e-5
 FLOPS = 2 * TOK * D * D * 2 + 2 * TOK * H * HK * HV
 
 PIN = True
-D_ON_ACT = ()
+D_ON_ACT = (0, 1, 2)
 G_ON_POOL_MOD = 1
 
 
@@ -67,6 +67,11 @@ def tile_glamemoryreader_pb_t_kernel(
             w_codes[nm] = const.tile([P, D], U32, name="wc_" + nm, tag="wc_" + nm, align_bytes=64)
             w_scales[nm] = const.tile([P, D], U8, name="ws_" + nm, tag="ws_" + nm, align_bytes=64)
 
+        sq = []
+        for k in range(3):
+            sq.append(const.tile([P, 5, HV + 1], F32, name="sq%d" % k, tag="sq%d" % k))
+            nc.vector.memset(sq[k][:], 0.0)
+            nc.vector.memset(sq[k][:, :, HV : HV + 1], EPS)
         nc.gpsimd.memset(vecrows[:], 0.0)
         nc.vector.memset(eps_t[:], EPS)
         nc.vector.memset(neghalf[:], -0.5)
@@ -137,8 +142,7 @@ def tile_glamemoryreader_pb_t_kernel(
                 nc.vector.quantize_mx(out=w_codes[nm][:, sl].bitcast(FP8X4), scales=w_scales[nm][:, sl], in_=wg[:])
 
         def stat_tiles(s):
-            if s not in ms:
-                ms[s] = stat.tile([P, 8], F32, name="ms%d" % s, tag="ms")
+            if s not in vv:
                 vv[s] = stat.tile([P, 8], F32, name="vv%d" % s, tag="vv")
                 rs[s] = stat.tile([P, 8], F32, name="rs%d" % s, tag="rs")
 
@@ -163,7 +167,7 @@ def tile_glamemoryreader_pb_t_kernel(
             if ok(i) and i % 2 == 0:
                 u = i // 2
                 qT[u] = qtp.tile([P, 2, H, P], BF16, name="qT%d" % u, tag="qT")
-                nc.vector.tensor_copy(out=qT[u][:], in_=qTp[u][:])
+                nc.scalar.copy(out=qT[u][:], in_=qTp[u][:])
 
         def op_mr(i):
             if ok(i):
@@ -180,38 +184,33 @@ def tile_glamemoryreader_pb_t_kernel(
 
         def op_f(i):
             if ok(i):
-                stat_tiles(i)
                 nc.scalar.activation(
                     out=junk[:],
                     in_=h_t[i // GT][:, i % GT, :],
                     func=ACTF.Square,
                     scale=1.0 / math.sqrt(D),
-                    accum_out=ms[i][:, 4:5],
+                    accum_out=sq[i % 3][:, 4, 0:1],
                 )
 
         def op_b(i):
             if ok(i):
-                stat_tiles(i + 2)
-                for h in range(H):
-                    nc.scalar.activation(
-                        out=junk[:, 0:HV],
-                        in_=r_ps[i][:, h * HV : (h + 1) * HV],
-                        func=ACTF.Square,
-                        scale=1.0 / math.sqrt(HV),
-                        accum_out=ms[i + 2][:, h : h + 1],
-                    )
+                nc.scalar.activation(
+                    out=sq[(i + 2) % 3][:, 0:H, 0:HV],
+                    in_=r_ps[i][:].rearrange("p (h v) -> p h v", h=H),
+                    func=ACTF.Square,
+                    scale=1.0 / math.sqrt(HV),
+                )
 
-        def op_eps(s):
+        def op_red(s):
             lo, hi = stat_range(s)
             if lo < hi:
-                nc.scalar.activation(
-                    out=vv[s][:, lo:hi], in_=ms[s][:, lo:hi], func=ACTF.Identity, bias=eps_t[:, 0:1], scale=1.0
-                )
+                stat_tiles(s)
+                nc.vector.tensor_reduce(out=vv[s][:, 0:5], in_=sq[s % 3][:], axis=mybir.AxisListType.X, op=ALU.add)
 
         def op_pow(s):
             lo, hi = stat_range(s)
             if lo < hi:
-                nc.gpsimd.tensor_tensor(out=rs[s][:, lo:hi], in0=vv[s][:, lo:hi], in1=neghalf[:, lo:hi], op=ALU.pow)
+                nc.gpsimd.tensor_tensor(out=rs[s][:, 0:5], in0=vv[s][:, 0:5], in1=neghalf[:, 0:5], op=ALU.pow)
 
         def op_g(i):
             if ok(i):
@@ -319,10 +318,12 @@ def tile_glamemoryreader_pb_t_kernel(
                 if i % GT == 0:
                     o_t[g] = ob.tile([P, GT, D], F32, name="o%d" % g, tag="o")
                 nc.vector.tensor_tensor(out=o_t[g][:, i % GT, :], in0=p_ps[i][:], in1=gate[i][:], op=ALU.mult)
-                if i % GT == GT - 1:
+                if g == NG - 1:
+                    nc.sync.dma_start(out=grp(os_, g)[:, i % GT, :], in_=o_t[g][:, i % GT, :])
+                elif i % GT == GT - 1:
                     nc.sync.dma_start(out=grp(os_, g), in_=o_t[g][:])
 
-        for tau in range(-12, NT + 6):
+        for tau in range(-12, NT + 7):
             if (tau + 12) % GT == 0 and (tau + 12) // GT < NG:
                 load((tau + 12) // GT)
             if tau == -3:
@@ -337,16 +338,16 @@ def tile_glamemoryreader_pb_t_kernel(
             op_pow(tau + 1)
             op_b(tau)
             op_j(tau - 4)
-            op_mxp(tau - 5)
+            op_mxp(tau - 6)
             op_tn(tau - 3)
-            op_k(tau - 5)
+            op_k(tau - 6)
             op_tq(tau + 4)
             op_a(tau + 3)
             op_d(tau - 3)
             op_tx(tau - 1)
             op_i(tau - 2)
             op_mr(tau + 1)
-            op_e(tau - 3)
+            op_e(tau - 4)
+            op_red(tau + 2)
             op_g(tau)
             op_mxg(tau - 3)
-            op_eps(tau + 2)

@@ -20,11 +20,10 @@ GT = 4
 NG = NT // GT
 EPS = 1e-5
 
-FLOPS = 2 * TOK * D * D * 2 + 2 * TOK * H * HK * HV
+X_ON_POOL = (0,)
+X_MOD = 2
 
-PIN = True
-D_ON_ACT = (0, 1, 2)
-G_ON_POOL_MOD = 1
+FLOPS = 2 * TOK * D * D * 2 + 2 * TOK * H * HK * HV
 
 
 def tile_glamemoryreader_pb_t_kernel(
@@ -41,43 +40,38 @@ def tile_glamemoryreader_pb_t_kernel(
         ob = ctx.enter_context(tc.tile_pool(name="ob", bufs=3))
         mid = ctx.enter_context(tc.tile_pool(name="mid", bufs=4))
         qtp = ctx.enter_context(tc.tile_pool(name="qtp", bufs=3))
-        cod = ctx.enter_context(tc.tile_pool(name="cod", bufs=5))
+        cod = ctx.enter_context(tc.tile_pool(name="cod", bufs=4))
         stat = ctx.enter_context(tc.tile_pool(name="stat", bufs=8))
-        psum1 = ctx.enter_context(tc.psum_pool(name="psum1", bufs=1))
+        psum_q = ctx.enter_context(tc.psum_pool(name="psumq", bufs=1))
         psum_r = ctx.enter_context(tc.psum_pool(name="psumr", bufs=3))
-        psum_t = ctx.enter_context(tc.psum_pool(name="psumt", bufs=2))
-        psum_o = ctx.enter_context(tc.psum_pool(name="psumo", bufs=2))
-        if PIN:
-            ctx.enter_context(tc.manual_schedule())
+        psum_t = ctx.enter_context(tc.psum_pool(name="psumt", bufs=1))
+        psum_o = ctx.enter_context(tc.psum_pool(name="psumo", bufs=3))
+        ctx.enter_context(tc.manual_schedule())
 
-        vecrows = const.tile([P, P], BF16, name="vecrows", tag="vecrows")
+        wrow = const.tile([P, D + HV], BF16, name="wrow", tag="wrow")
+        ones = const.tile([P, P], BF16, name="ones", tag="ones")
+        nw_bc = const.tile([P, D], BF16, name="nw_bc", tag="nw_bc")
+        vw_bc = const.tile([P, HV], BF16, name="vw_bc", tag="vw_bc")
         ident_b = const.tile([P, P], BF16, name="ident_b", tag="ident_b")
         ident_f = const.tile([P, P], F32, name="ident_f", tag="ident_f")
-        eps_t = const.tile([P, 1], F32, name="eps_t", tag="eps_t")
         neghalf = const.tile([P, 8], F32, name="neghalf", tag="neghalf")
         scr = const.tile([P, 1], F32, name="scr", tag="scr")
-        cols = const.tile([P, 8], F32, name="cols", tag="cols")
         junk = const.tile([P, D], BF16, name="junk", tag="junk")
         s_sb = const.tile([P, B * H, HV], BF16, name="s_sb", tag="s_sb")
         w_raw = {}
         w_codes = {}
         w_scales = {}
         for nm in ("g", "o"):
-            w_raw[nm] = const.tile([P, 16, P], BF16, name="wraw_" + nm, tag="wraw_" + nm)
+            w_raw[nm] = const.tile([P, 4, D], BF16, name="wraw_" + nm, tag="wraw_" + nm)
             w_codes[nm] = const.tile([P, D], U32, name="wc_" + nm, tag="wc_" + nm, align_bytes=64)
             w_scales[nm] = const.tile([P, D], U8, name="ws_" + nm, tag="ws_" + nm, align_bytes=64)
 
-        sq = []
-        for k in range(3):
-            sq.append(const.tile([P, 5, HV + 1], F32, name="sq%d" % k, tag="sq%d" % k))
-            nc.vector.memset(sq[k][:], 0.0)
-            nc.vector.memset(sq[k][:, :, HV : HV + 1], EPS)
-        nc.gpsimd.memset(vecrows[:], 0.0)
-        nc.vector.memset(eps_t[:], EPS)
+        nc.vector.memset(wrow[:], 0.0)
+        nc.vector.memset(ones[:], 1.0)
         nc.vector.memset(neghalf[:], -0.5)
-        nc.scalar.dma_start(out=vecrows[0:4, :], in_=norm_w.rearrange("(j c) -> j c", c=P))
-        nc.scalar.dma_start(out=vecrows[4:5, :], in_=v_norm_w.rearrange("(o c) -> o c", o=1))
-        nc.scalar.activation(out=scr[:], in_=eps_t[:], func=ACTF.Sigmoid)
+        nc.scalar.dma_start(out=wrow[0:1, 0:D], in_=norm_w.rearrange("(o c) -> o c", o=1))
+        nc.scalar.dma_start(out=wrow[0:1, D : D + HV], in_=v_norm_w.rearrange("(o c) -> o c", o=1))
+        nc.scalar.activation(out=scr[:], in_=neghalf[:, 0:1], func=ACTF.Sigmoid)
         make_identity(nc, ident_b[:])
         make_identity(nc, ident_f[:])
 
@@ -90,16 +84,13 @@ def tile_glamemoryreader_pb_t_kernel(
         ms = {}
         vv = {}
         rs = {}
-        yx = {}
-        yn = {}
-        xT = {}
-        nT = {}
-        xg = {}
-        ng = {}
-        xc = {}
-        xs = {}
-        ncd = {}
-        nsc = {}
+        hw = {}
+        xb = {}
+        nb = {}
+        tp = {}
+        xng = {}
+        xnc = {}
+        xns = {}
         g_ps = {}
         p_ps = {}
         gate = {}
@@ -118,43 +109,33 @@ def tile_glamemoryreader_pb_t_kernel(
             if g == 0:
                 nc.sync.dma_start(out=s_sb[:], in_=recurrent_state.rearrange("b h k v -> k (b h) v"))
                 for nm, w in (("g", gate_w), ("o", o_w)):
-                    nc.sync.dma_start(
-                        out=w_raw[nm][:],
-                        in_=w.rearrange("d (j c) -> (d j) c", c=P).rearrange("(k a) c -> a k c", a=P),
-                    )
+                    nc.sync.dma_start(out=w_raw[nm][:], in_=w.rearrange("(a p) k -> p a k", p=P))
 
         def prep_vec():
-            vps = psum_t.tile([P, P], BF16, name="vps", tag="T")
-            nc.tensor.transpose(vps[:], vecrows[:], ident_b[:])
-            nc.vector.tensor_copy(out=cols[:, 0:5], in_=vps[:, 0:5])
+            a_ps = psum_o.tile([P, D], F32, name="nw_ps", tag="O")
+            nc.tensor.matmul(out=a_ps[:], lhsT=ones[:], rhs=wrow[:, 0:D], start=True, stop=True)
+            nc.vector.tensor_copy(out=nw_bc[:], in_=a_ps[:])
+            b_ps = psum_o.tile([P, D], F32, name="vw_ps", tag="O")
+            nc.tensor.matmul(out=b_ps[:, 0:HV], lhsT=ones[:], rhs=wrow[:, D : D + HV], start=True, stop=True)
+            nc.vector.tensor_copy(out=vw_bc[:], in_=b_ps[:, 0:HV])
 
         def prep_weight(nm):
+            words = w_raw[nm][:].bitcast(F32)
             for half in range(2):
-                wps = psum_o.tile([P, 1024], BF16, name="wps_%s%d" % (nm, half), tag="O")
-                for k in range(8):
-                    nc.tensor.transpose(wps[:, k * P : (k + 1) * P], w_raw[nm][:, half * 8 + k, :], ident_b[:])
+                wps = psum_o.tile([P, 2, 2, P], F32, name="wps_%s%d" % (nm, half), tag="O")
+                for k in range(2):
+                    for u in range(2):
+                        nc.tensor.transpose(wps[:, k, u, :], words[:, half * 2 + k, u * P : (u + 1) * P], ident_f[:])
                 wg = const.tile([P, 1024], BF16, name="wg_%s%d" % (nm, half), tag="wg_%s%d" % (nm, half), align_bytes=64)
-                if half == 0:
-                    nc.scalar.copy(out=wg[:], in_=wps[:])
-                else:
-                    nc.vector.tensor_copy(out=wg[:], in_=wps[:])
+                dst = wg[:].bitcast(F32).rearrange("p (a t u) -> p a t u", a=2, u=2)
+                nc.vector.tensor_copy(out=dst, in_=wps[:].rearrange("p a u t -> p a t u"))
                 sl = slice(half * 256, (half + 1) * 256)
                 nc.vector.quantize_mx(out=w_codes[nm][:, sl].bitcast(FP8X4), scales=w_scales[nm][:, sl], in_=wg[:])
-
-        def stat_tiles(s):
-            if s not in vv:
-                vv[s] = stat.tile([P, 8], F32, name="vv%d" % s, tag="vv")
-                rs[s] = stat.tile([P, 8], F32, name="rs%d" % s, tag="rs")
-
-        def stat_range(s):
-            lo = 0 if ok(s - 2) else 4
-            hi = 5 if ok(s) else 4
-            return lo, hi
 
         def op_tq(i):
             if ok(i) and i % 2 == 0:
                 u = i // 2
-                qTp[u] = psum1.tile([P, 2, H, P], BF16, name="qTp%d" % u, tag="qTp")
+                qTp[u] = psum_q.tile([P, 2, H, P], BF16, name="qTp%d" % u, tag="qTp")
                 for half in range(2):
                     for h in range(H):
                         nc.tensor.transpose(
@@ -184,128 +165,111 @@ def tile_glamemoryreader_pb_t_kernel(
 
         def op_f(i):
             if ok(i):
+                vv[i] = stat.tile([P, 8], F32, name="vv%d" % i, tag="vv")
                 nc.scalar.activation(
                     out=junk[:],
                     in_=h_t[i // GT][:, i % GT, :],
                     func=ACTF.Square,
                     scale=1.0 / math.sqrt(D),
-                    accum_out=sq[i % 3][:, 4, 0:1],
+                    accum_out=vv[i][:, 4:5],
                 )
 
         def op_b(i):
             if ok(i):
-                nc.scalar.activation(
-                    out=sq[(i + 2) % 3][:, 0:H, 0:HV],
-                    in_=r_ps[i][:].rearrange("p (h v) -> p h v", h=H),
-                    func=ACTF.Square,
-                    scale=1.0 / math.sqrt(HV),
+                for h in range(H):
+                    nc.scalar.activation(
+                        out=junk[:, 0:HV],
+                        in_=r_ps[i][:, h * HV : (h + 1) * HV],
+                        func=ACTF.Square,
+                        scale=1.0 / math.sqrt(HV),
+                        accum_out=vv[i][:, h : h + 1],
+                    )
+
+        def op_pow(i):
+            if ok(i):
+                ms[i] = stat.tile([P, 8], F32, name="ms%d" % i, tag="ms")
+                rs[i] = stat.tile([P, 8], F32, name="rs%d" % i, tag="rs")
+                nc.gpsimd.tensor_scalar(
+                    out=ms[i][:, 0:5], in0=vv[i][:, 0:5], scalar1=1.0, scalar2=EPS, op0=ALU.mult, op1=ALU.add
+                )
+                nc.gpsimd.tensor_tensor(out=rs[i][:, 0:5], in0=ms[i][:, 0:5], in1=neghalf[:, 0:5], op=ALU.pow)
+
+        def op_u(i):
+            if ok(i) and i % X_MOD in X_ON_POOL:
+                hw[i] = mid.tile([P, D], F32, name="hw%d" % i, tag="hw")
+                nc.gpsimd.tensor_tensor(out=hw[i][:], in0=h_t[i // GT][:, i % GT, :], in1=nw_bc[:], op=ALU.mult)
+
+        def op_xv(i):
+            if ok(i) and i % X_MOD not in X_ON_POOL:
+                xb[i] = mid.tile([P, D], BF16, name="xb%d" % i, tag="xb")
+                nc.vector.scalar_tensor_tensor(
+                    out=xb[i][:],
+                    in0=h_t[i // GT][:, i % GT, :],
+                    scalar=rs[i][:, 4:5],
+                    in1=nw_bc[:],
+                    op0=ALU.mult,
+                    op1=ALU.mult,
                 )
 
-        def op_red(s):
-            lo, hi = stat_range(s)
-            if lo < hi:
-                stat_tiles(s)
-                nc.vector.tensor_reduce(out=vv[s][:, 0:5], in_=sq[s % 3][:], axis=mybir.AxisListType.X, op=ALU.add)
-
-        def op_pow(s):
-            lo, hi = stat_range(s)
-            if lo < hi:
-                nc.gpsimd.tensor_tensor(out=rs[s][:, 0:5], in0=vv[s][:, 0:5], in1=neghalf[:, 0:5], op=ALU.pow)
-
         def op_g(i):
-            if ok(i):
-                yx[i] = mid.tile([P, D], F32, name="yx%d" % i, tag="yx")
-                if i % G_ON_POOL_MOD == 0:
-                    nc.gpsimd.tensor_scalar(
-                        out=yx[i][:],
-                        in0=h_t[i // GT][:, i % GT, :],
-                        scalar1=rs[i][:, 4:5],
-                        scalar2=0.0,
-                        op0=ALU.mult,
-                        op1=ALU.add,
-                    )
-                else:
-                    nc.vector.tensor_scalar(
-                        out=yx[i][:], in0=h_t[i // GT][:, i % GT, :], scalar1=rs[i][:, 4:5], scalar2=None, op0=ALU.mult
-                    )
+            if ok(i) and i % X_MOD in X_ON_POOL:
+                xb[i] = mid.tile([P, D], BF16, name="xb%d" % i, tag="xb")
+                nc.gpsimd.tensor_scalar(
+                    out=xb[i][:], in0=hw[i][:], scalar1=rs[i][:, 4:5], scalar2=0.0, op0=ALU.mult, op1=ALU.add
+                )
 
         def op_c(i):
             if ok(i):
-                yn[i] = mid.tile([P, H, HV], F32, name="yn%d" % i, tag="yn")
-                nc.vector.tensor_tensor(
-                    out=yn[i][:],
-                    in0=r_ps[i][:].rearrange("p (h v) -> p h v", h=H),
-                    in1=rs[i + 2][:, 0:H].unsqueeze(2).to_broadcast([P, H, HV]),
-                    op=ALU.mult,
-                )
+                nb[i] = mid.tile([P, D], BF16, name="nb%d" % i, tag="nb")
+                for h in range(H):
+                    sl = slice(h * HV, (h + 1) * HV)
+                    nc.vector.scalar_tensor_tensor(
+                        out=nb[i][:, sl],
+                        in0=r_ps[i][:, sl],
+                        scalar=rs[i][:, h : h + 1],
+                        in1=vw_bc[:],
+                        op0=ALU.mult,
+                        op1=ALU.mult,
+                    )
 
-        def op_tx(i):
+        def op_t(i):
             if ok(i):
-                xT[i] = psum_t.tile([P, 4, P], F32, name="xT%d" % i, tag="T")
-                for j in range(4):
-                    nc.tensor.transpose(xT[i][:, j, :], yx[i][:, j * P : (j + 1) * P], ident_f[:])
-
-        def op_tn(i):
-            if ok(i):
-                nT[i] = psum_t.tile([P, 4, P], F32, name="nT%d" % i, tag="T")
-                for j in range(4):
-                    nc.tensor.transpose(nT[i][:, j, :], yn[i][:, j, :], ident_f[:])
-
-        def op_h(i):
-            if ok(i):
-                xg[i] = mid.tile([P, P, 4], BF16, name="xg%d" % i, tag="xg", align_bytes=64)
-                nc.vector.tensor_tensor(
-                    out=xg[i][:],
-                    in0=xT[i][:].rearrange("p j t -> p t j"),
-                    in1=cols[:, 0:4].unsqueeze(1).to_broadcast([P, P, 4]),
-                    op=ALU.mult,
-                )
+                tp[i] = psum_t.tile([P, 2, 2, P], F32, name="tp%d" % i, tag="T")
+                for c, src in enumerate((xb[i], nb[i])):
+                    words = src[:].bitcast(F32)
+                    for u in range(2):
+                        nc.tensor.transpose(tp[i][:, c, u, :], words[:, u * P : (u + 1) * P], ident_f[:])
 
         def op_d(i):
             if ok(i):
-                ng[i] = mid.tile([P, P, 4], BF16, name="ng%d" % i, tag="ng", align_bytes=64)
-                src = nT[i][:].rearrange("p j t -> p t j")
-                if i % 3 in D_ON_ACT:
-                    nc.scalar.activation(out=ng[i][:], in_=src, func=ACTF.Copy, scale=cols[:, 4:5])
-                else:
-                    nc.vector.tensor_scalar(out=ng[i][:], in0=src, scalar1=cols[:, 4:5], scalar2=None, op0=ALU.mult)
-
-        def op_i(i):
-            if ok(i):
-                xc[i] = cod.tile([P, P], U32, name="xc%d" % i, tag="xc", align_bytes=64)
-                xs[i] = cod.tile([P, P], U8, name="xs%d" % i, tag="xs", align_bytes=64)
-                nc.vector.quantize_mx(
-                    out=xc[i][:].bitcast(FP8X4), scales=xs[i][:], in_=xg[i][:].rearrange("p t j -> p (t j)")
-                )
+                xng[i] = mid.tile([P, 1024], BF16, name="xng%d" % i, tag="xng", align_bytes=64)
+                dst = xng[i][:].bitcast(F32).rearrange("p (c t u) -> p c t u", c=2, u=2)
+                nc.vector.tensor_copy(out=dst, in_=tp[i][:].rearrange("p c u t -> p c t u"))
 
         def op_e(i):
             if ok(i):
-                ncd[i] = cod.tile([P, P], U32, name="nc%d" % i, tag="nc", align_bytes=64)
-                nsc[i] = cod.tile([P, P], U8, name="ns%d" % i, tag="ns", align_bytes=64)
-                nc.vector.quantize_mx(
-                    out=ncd[i][:].bitcast(FP8X4), scales=nsc[i][:], in_=ng[i][:].rearrange("p t j -> p (t j)")
-                )
+                xnc[i] = cod.tile([P, 256], U32, name="xnc%d" % i, tag="xnc", align_bytes=64)
+                xns[i] = cod.tile([P, 256], U8, name="xns%d" % i, tag="xns", align_bytes=64)
+                nc.vector.quantize_mx(out=xnc[i][:].bitcast(FP8X4), scales=xns[i][:], in_=xng[i][:])
 
-        def mx(dst, codes, scales, nm):
+        def mx(dst, i, c, nm):
+            sl = slice(c * P, (c + 1) * P)
             nc.tensor.matmul_mx(
                 out=dst[:],
-                lhsT=codes[:].bitcast(FP8X4),
-                lhsT_scale=scales[:],
+                lhsT=xnc[i][:, sl].bitcast(FP8X4),
+                lhsT_scale=xns[i][:, sl],
                 rhs=w_codes[nm][:].bitcast(FP8X4),
                 rhs_scale=w_scales[nm][:],
                 start=True,
                 stop=True,
             )
 
-        def op_mxg(i):
+        def op_mx(i):
             if ok(i):
                 g_ps[i] = psum_o.tile([P, D], F32, name="g%d" % i, tag="O")
-                mx(g_ps[i], xc[i], xs[i], "g")
-
-        def op_mxp(i):
-            if ok(i):
+                mx(g_ps[i], i, 0, "g")
                 p_ps[i] = psum_o.tile([P, D], F32, name="p%d" % i, tag="O")
-                mx(p_ps[i], ncd[i], nsc[i], "o")
+                mx(p_ps[i], i, 1, "o")
 
         def op_j(i):
             if ok(i):
@@ -323,31 +287,28 @@ def tile_glamemoryreader_pb_t_kernel(
                 elif i % GT == GT - 1:
                     nc.sync.dma_start(out=grp(os_, g), in_=o_t[g][:])
 
-        for tau in range(-12, NT + 7):
-            if (tau + 12) % GT == 0 and (tau + 12) // GT < NG:
-                load((tau + 12) // GT)
-            if tau == -3:
+        for s in range(-10, NT + 6):
+            if (s + 10) % GT == 0 and (s + 10) // GT < NG:
+                load((s + 10) // GT)
+            if s == -3:
                 prep_vec()
-            if tau == 1:
+            if s == 1:
                 prep_weight("g")
-            if tau == 2:
+            if s == 2:
                 prep_weight("o")
-            op_f(tau + 2)
-            op_h(tau - 2)
-            op_c(tau - 2)
-            op_pow(tau + 1)
-            op_b(tau)
-            op_j(tau - 4)
-            op_mxp(tau - 6)
-            op_tn(tau - 3)
-            op_k(tau - 6)
-            op_tq(tau + 4)
-            op_a(tau + 3)
-            op_d(tau - 3)
-            op_tx(tau - 1)
-            op_i(tau - 2)
-            op_mr(tau + 1)
-            op_e(tau - 4)
-            op_red(tau + 2)
-            op_g(tau)
-            op_mxg(tau - 3)
+            op_g(s - 2)
+            op_c(s - 3)
+            op_t(s - 3)
+            op_b(s - 1)
+            op_j(s - 5)
+            op_e(s - 4)
+            op_xv(s - 2)
+            op_k(s - 5)
+            op_d(s - 3)
+            op_f(s)
+            op_pow(s - 1)
+            op_u(s - 1)
+            op_mr(s)
+            op_tq(s + 2)
+            op_a(s + 1)
+            op_mx(s - 4)

@@ -20,8 +20,8 @@ GT = 4
 NG = NT // GT
 EPS = 1e-5
 
-X_ON_POOL = (0,)
-X_MOD = 2
+D_MOD = 2
+D_ON_ACT = (1,)
 
 FLOPS = 2 * TOK * D * D * 2 + 2 * TOK * H * HK * HV
 
@@ -43,8 +43,8 @@ def tile_glamemoryreader_pb_t_kernel(
         cod = ctx.enter_context(tc.tile_pool(name="cod", bufs=4))
         stat = ctx.enter_context(tc.tile_pool(name="stat", bufs=8))
         psum_q = ctx.enter_context(tc.psum_pool(name="psumq", bufs=1))
-        psum_r = ctx.enter_context(tc.psum_pool(name="psumr", bufs=3))
-        psum_t = ctx.enter_context(tc.psum_pool(name="psumt", bufs=1))
+        psum_r = ctx.enter_context(tc.psum_pool(name="psumr", bufs=2))
+        psum_t = ctx.enter_context(tc.psum_pool(name="psumt", bufs=2))
         psum_o = ctx.enter_context(tc.psum_pool(name="psumo", bufs=3))
         ctx.enter_context(tc.manual_schedule())
 
@@ -84,7 +84,6 @@ def tile_glamemoryreader_pb_t_kernel(
         ms = {}
         vv = {}
         rs = {}
-        hw = {}
         xb = {}
         nb = {}
         tp = {}
@@ -194,13 +193,8 @@ def tile_glamemoryreader_pb_t_kernel(
                 )
                 nc.gpsimd.tensor_tensor(out=rs[i][:, 0:5], in0=ms[i][:, 0:5], in1=neghalf[:, 0:5], op=ALU.pow)
 
-        def op_u(i):
-            if ok(i) and i % X_MOD in X_ON_POOL:
-                hw[i] = mid.tile([P, D], F32, name="hw%d" % i, tag="hw")
-                nc.gpsimd.tensor_tensor(out=hw[i][:], in0=h_t[i // GT][:, i % GT, :], in1=nw_bc[:], op=ALU.mult)
-
         def op_xv(i):
-            if ok(i) and i % X_MOD not in X_ON_POOL:
+            if ok(i):
                 xb[i] = mid.tile([P, D], BF16, name="xb%d" % i, tag="xb")
                 nc.vector.scalar_tensor_tensor(
                     out=xb[i][:],
@@ -209,13 +203,6 @@ def tile_glamemoryreader_pb_t_kernel(
                     in1=nw_bc[:],
                     op0=ALU.mult,
                     op1=ALU.mult,
-                )
-
-        def op_g(i):
-            if ok(i) and i % X_MOD in X_ON_POOL:
-                xb[i] = mid.tile([P, D], BF16, name="xb%d" % i, tag="xb")
-                nc.gpsimd.tensor_scalar(
-                    out=xb[i][:], in0=hw[i][:], scalar1=rs[i][:, 4:5], scalar2=0.0, op0=ALU.mult, op1=ALU.add
                 )
 
         def op_c(i):
@@ -244,7 +231,11 @@ def tile_glamemoryreader_pb_t_kernel(
             if ok(i):
                 xng[i] = mid.tile([P, 1024], BF16, name="xng%d" % i, tag="xng", align_bytes=64)
                 dst = xng[i][:].bitcast(F32).rearrange("p (c t u) -> p c t u", c=2, u=2)
-                nc.vector.tensor_copy(out=dst, in_=tp[i][:].rearrange("p c u t -> p c t u"))
+                src = tp[i][:].rearrange("p c u t -> p c t u")
+                if i % D_MOD in D_ON_ACT:
+                    nc.scalar.copy(out=dst, in_=src)
+                else:
+                    nc.vector.tensor_copy(out=dst, in_=src)
 
         def op_e(i):
             if ok(i):
@@ -287,28 +278,25 @@ def tile_glamemoryreader_pb_t_kernel(
                 elif i % GT == GT - 1:
                     nc.sync.dma_start(out=grp(os_, g), in_=o_t[g][:])
 
-        for s in range(-10, NT + 6):
-            if (s + 10) % GT == 0 and (s + 10) // GT < NG:
-                load((s + 10) // GT)
+        for s in range(-12, NT + 2):
+            if (s + 12) % GT == 0 and (s + 12) // GT < NG:
+                load((s + 12) // GT)
             if s == -3:
                 prep_vec()
-            if s == 1:
+            if s == 0:
                 prep_weight("g")
-            if s == 2:
                 prep_weight("o")
-            op_g(s - 2)
-            op_c(s - 3)
-            op_t(s - 3)
-            op_b(s - 1)
-            op_j(s - 5)
-            op_e(s - 4)
-            op_xv(s - 2)
-            op_k(s - 5)
-            op_d(s - 3)
-            op_f(s)
-            op_pow(s - 1)
-            op_u(s - 1)
-            op_mr(s)
-            op_tq(s + 2)
-            op_a(s + 1)
-            op_mx(s - 4)
+            op_c(s)
+            op_e(s - 1)
+            op_xv(s + 1)
+            op_mr(s + 2)
+            op_t(s)
+            op_tq(s + 4)
+            op_mx(s - 1)
+            op_b(s + 2)
+            op_f(s + 3)
+            op_pow(s + 2)
+            op_a(s + 3)
+            op_d(s)
+            op_j(s - 1)
+            op_k(s - 2)

@@ -42,21 +42,23 @@ def tile_glamemoryreader_pb_t_kernel(
         qtp = ctx.enter_context(tc.tile_pool(name="qtp", bufs=3))
         cod = ctx.enter_context(tc.tile_pool(name="cod", bufs=4))
         stat = ctx.enter_context(tc.tile_pool(name="stat", bufs=8))
+        psum_w = ctx.enter_context(tc.psum_pool(name="psumw", bufs=1))
         psum_q = ctx.enter_context(tc.psum_pool(name="psumq", bufs=1))
-        psum_r = ctx.enter_context(tc.psum_pool(name="psumr", bufs=2))
-        psum_t = ctx.enter_context(tc.psum_pool(name="psumt", bufs=2))
-        psum_o = ctx.enter_context(tc.psum_pool(name="psumo", bufs=3))
+        psum_r = ctx.enter_context(tc.psum_pool(name="psumr", bufs=3))
+        psum_t = ctx.enter_context(tc.psum_pool(name="psumt", bufs=1))
+        psum_o = ctx.enter_context(tc.psum_pool(name="psumo", bufs=2))
         ctx.enter_context(tc.manual_schedule())
 
         wrow = const.tile([P, D + HV], BF16, name="wrow", tag="wrow")
         ones = const.tile([P, P], BF16, name="ones", tag="ones")
-        nw_bc = const.tile([P, D], BF16, name="nw_bc", tag="nw_bc")
+        nw_bc = psum_w.tile([P, D], F32, name="nw_bc", tag="nw_bc")
         vw_bc = const.tile([P, HV], BF16, name="vw_bc", tag="vw_bc")
         ident_b = const.tile([P, P], BF16, name="ident_b", tag="ident_b")
         ident_f = const.tile([P, P], F32, name="ident_f", tag="ident_f")
         neghalf = const.tile([P, 8], F32, name="neghalf", tag="neghalf")
         scr = const.tile([P, 1], F32, name="scr", tag="scr")
-        junk = const.tile([P, D], BF16, name="junk", tag="junk")
+        junk_h = const.tile([P, D], BF16, name="junk_h", tag="junk_h")
+        junk_r = const.tile([P, D], BF16, name="junk_r", tag="junk_r")
         s_sb = const.tile([P, B * H, HV], BF16, name="s_sb", tag="s_sb")
         w_raw = {}
         w_codes = {}
@@ -111,9 +113,7 @@ def tile_glamemoryreader_pb_t_kernel(
                     nc.sync.dma_start(out=w_raw[nm][:], in_=w.rearrange("(a p) k -> p a k", p=P))
 
         def prep_vec():
-            a_ps = psum_o.tile([P, D], F32, name="nw_ps", tag="O")
-            nc.tensor.matmul(out=a_ps[:], lhsT=ones[:], rhs=wrow[:, 0:D], start=True, stop=True)
-            nc.vector.tensor_copy(out=nw_bc[:], in_=a_ps[:])
+            nc.tensor.matmul(out=nw_bc[:], lhsT=ones[:], rhs=wrow[:, 0:D], start=True, stop=True)
             b_ps = psum_o.tile([P, D], F32, name="vw_ps", tag="O")
             nc.tensor.matmul(out=b_ps[:, 0:HV], lhsT=ones[:], rhs=wrow[:, D : D + HV], start=True, stop=True)
             nc.vector.tensor_copy(out=vw_bc[:], in_=b_ps[:, 0:HV])
@@ -166,7 +166,7 @@ def tile_glamemoryreader_pb_t_kernel(
             if ok(i):
                 vv[i] = stat.tile([P, 8], F32, name="vv%d" % i, tag="vv")
                 nc.scalar.activation(
-                    out=junk[:],
+                    out=junk_h[:],
                     in_=h_t[i // GT][:, i % GT, :],
                     func=ACTF.Square,
                     scale=1.0 / math.sqrt(D),
@@ -177,7 +177,7 @@ def tile_glamemoryreader_pb_t_kernel(
             if ok(i):
                 for h in range(H):
                     nc.scalar.activation(
-                        out=junk[:, 0:HV],
+                        out=junk_r[:, h * HV : (h + 1) * HV],
                         in_=r_ps[i][:, h * HV : (h + 1) * HV],
                         func=ACTF.Square,
                         scale=1.0 / math.sqrt(HV),
@@ -278,25 +278,26 @@ def tile_glamemoryreader_pb_t_kernel(
                 elif i % GT == GT - 1:
                     nc.sync.dma_start(out=grp(os_, g), in_=o_t[g][:])
 
-        for s in range(-12, NT + 2):
-            if (s + 12) % GT == 0 and (s + 12) // GT < NG:
-                load((s + 12) // GT)
+        for s in range(-10, NT + 6):
+            if (s + 10) % GT == 0 and (s + 10) // GT < NG:
+                load((s + 10) // GT)
             if s == -3:
                 prep_vec()
-            if s == 0:
+            if s == 1:
                 prep_weight("g")
+            if s == 2:
                 prep_weight("o")
-            op_c(s)
-            op_e(s - 1)
-            op_xv(s + 1)
-            op_mr(s + 2)
-            op_t(s)
-            op_tq(s + 4)
-            op_mx(s - 1)
-            op_b(s + 2)
-            op_f(s + 3)
-            op_pow(s + 2)
-            op_a(s + 3)
-            op_d(s)
-            op_j(s - 1)
-            op_k(s - 2)
+            op_b(s - 1)
+            op_j(s - 5)
+            op_c(s - 3)
+            op_e(s - 4)
+            op_t(s - 3)
+            op_f(s + 1)
+            op_mr(s)
+            op_xv(s - 2)
+            op_d(s - 3)
+            op_pow(s - 1)
+            op_tq(s + 2)
+            op_k(s - 5)
+            op_a(s + 1)
+            op_mx(s - 4)

@@ -71,8 +71,6 @@ def tile_glamemoryreader_pb_t_kernel(
         nc.vector.memset(wrow[:], 0.0)
         nc.vector.memset(ones[:], 1.0)
         nc.vector.memset(neghalf[:], -0.5)
-        nc.scalar.dma_start(out=wrow[0:1, 0:D], in_=norm_w.rearrange("(o c) -> o c", o=1))
-        nc.scalar.dma_start(out=wrow[0:1, D : D + HV], in_=v_norm_w.rearrange("(o c) -> o c", o=1))
         nc.scalar.activation(out=scr[:], in_=neghalf[:, 0:1], func=ACTF.Sigmoid)
         make_identity(nc, ident_b[:])
         make_identity(nc, ident_f[:])
@@ -104,13 +102,23 @@ def tile_glamemoryreader_pb_t_kernel(
 
         def load(g):
             q_t[g] = io.tile([P, GT, D], BF16, name="q%d" % g, tag="q")
-            nc.sync.dma_start(out=q_t[g][:], in_=grp(qs, g))
             h_t[g] = io.tile([P, GT, D], BF16, name="h%d" % g, tag="h")
-            nc.sync.dma_start(out=h_t[g][:], in_=grp(hs, g))
-            if g == 0:
-                nc.sync.dma_start(out=s_sb[:], in_=recurrent_state.rearrange("b h k v -> k (b h) v"))
-                for nm, w in (("g", gate_w), ("o", o_w)):
-                    nc.sync.dma_start(out=w_raw[nm][:], in_=w.rearrange("(a p) k -> p a k", p=P))
+            if g > 0:
+                nc.sync.dma_start(out=q_t[g][:], in_=grp(qs, g))
+                nc.sync.dma_start(out=h_t[g][:], in_=grp(hs, g))
+            else:
+                first, second = slice(0, 2), slice(2, 4)
+                states = recurrent_state.rearrange("b h k v -> k (b h) v")
+                nc.sync.dma_start(out=q_t[g][:, first, :], in_=grp(qs, g)[:, first, :])
+                nc.sync.dma_start(out=h_t[g][:, first, :], in_=grp(hs, g)[:, first, :])
+                nc.sync.dma_start(out=s_sb[:, 0:H, :], in_=states[:, 0:H, :])
+                nc.sync.dma_start(out=w_raw["g"][:], in_=gate_w.rearrange("(a p) k -> p a k", p=P))
+                nc.sync.dma_start(out=wrow[0:1, 0:D], in_=norm_w.rearrange("(o c) -> o c", o=1))
+                nc.sync.dma_start(out=wrow[0:1, D : D + HV], in_=v_norm_w.rearrange("(o c) -> o c", o=1))
+                nc.sync.dma_start(out=q_t[g][:, second, :], in_=grp(qs, g)[:, second, :])
+                nc.sync.dma_start(out=h_t[g][:, second, :], in_=grp(hs, g)[:, second, :])
+                nc.sync.dma_start(out=w_raw["o"][:], in_=o_w.rearrange("(a p) k -> p a k", p=P))
+                nc.sync.dma_start(out=s_sb[:, H:, :], in_=states[:, H:, :])
 
         def prep_vec():
             nc.tensor.matmul(out=nw_bc[:], lhsT=ones[:], rhs=wrow[:, 0:D], start=True, stop=True)
@@ -281,10 +289,9 @@ def tile_glamemoryreader_pb_t_kernel(
         for s in range(-10, NT + 6):
             if (s + 10) % GT == 0 and (s + 10) // GT < NG:
                 load((s + 10) // GT)
-            if s == -3:
-                prep_vec()
             if s == 1:
                 prep_weight("g")
+                prep_vec()
             if s == 2:
                 prep_weight("o")
             op_b(s - 1)

@@ -110,14 +110,14 @@ def tile_glamemoryreader_pb_t_kernel(
                 first, second = slice(0, 2), slice(2, 4)
                 states = recurrent_state.rearrange("b h k v -> k (b h) v")
                 nc.sync.dma_start(out=q_t[g][:, first, :], in_=grp(qs, g)[:, first, :])
-                nc.sync.dma_start(out=h_t[g][:, first, :], in_=grp(hs, g)[:, first, :])
                 nc.sync.dma_start(out=s_sb[:, 0:H, :], in_=states[:, 0:H, :])
                 nc.sync.dma_start(out=w_raw["g"][:], in_=gate_w.rearrange("(a p) k -> p a k", p=P))
+                nc.sync.dma_start(out=h_t[g][:, first, :], in_=grp(hs, g)[:, first, :])
+                nc.sync.dma_start(out=w_raw["o"][:], in_=o_w.rearrange("(a p) k -> p a k", p=P))
                 nc.sync.dma_start(out=wrow[0:1, 0:D], in_=norm_w.rearrange("(o c) -> o c", o=1))
                 nc.sync.dma_start(out=wrow[0:1, D : D + HV], in_=v_norm_w.rearrange("(o c) -> o c", o=1))
                 nc.sync.dma_start(out=q_t[g][:, second, :], in_=grp(qs, g)[:, second, :])
                 nc.sync.dma_start(out=h_t[g][:, second, :], in_=grp(hs, g)[:, second, :])
-                nc.sync.dma_start(out=w_raw["o"][:], in_=o_w.rearrange("(a p) k -> p a k", p=P))
                 nc.sync.dma_start(out=s_sb[:, H:, :], in_=states[:, H:, :])
 
         def prep_vec():
@@ -289,17 +289,17 @@ def tile_glamemoryreader_pb_t_kernel(
         for s in range(-10, NT + 6):
             if (s + 10) % GT == 0 and (s + 10) // GT < NG:
                 load((s + 10) // GT)
-            if s == 1:
+            if s == -1:
                 prep_weight("g")
-                prep_vec()
-            if s == 2:
+            if s == 1:
                 prep_weight("o")
+                prep_vec()
             op_b(s - 1)
             op_j(s - 5)
             op_c(s - 3)
             op_e(s - 4)
             op_t(s - 3)
-            op_f(s + 1)
+            op_f(s)
             op_mr(s)
             op_xv(s - 2)
             op_d(s - 3)

@@ -20,8 +20,8 @@ GT = 4
 NG = NT // GT
 EPS = 1e-5
 
-D_MOD = 2
-D_ON_ACT = (1,)
+D_MOD = 5
+D_ON_ACT = (1, 3)
 
 FLOPS = 2 * TOK * D * D * 2 + 2 * TOK * H * HK * HV
 
@@ -42,6 +42,7 @@ def tile_glamemoryreader_pb_t_kernel(
         qtp = ctx.enter_context(tc.tile_pool(name="qtp", bufs=3))
         cod = ctx.enter_context(tc.tile_pool(name="cod", bufs=4))
         stat = ctx.enter_context(tc.tile_pool(name="stat", bufs=8))
+        rsp = ctx.enter_context(tc.tile_pool(name="rsp", bufs=2))
         psum_w = ctx.enter_context(tc.psum_pool(name="psumw", bufs=1))
         psum_q = ctx.enter_context(tc.psum_pool(name="psumq", bufs=1))
         psum_r = ctx.enter_context(tc.psum_pool(name="psumr", bufs=3))
@@ -195,7 +196,7 @@ def tile_glamemoryreader_pb_t_kernel(
         def op_pow(i):
             if ok(i):
                 ms[i] = stat.tile([P, 8], F32, name="ms%d" % i, tag="ms")
-                rs[i] = stat.tile([P, 8], F32, name="rs%d" % i, tag="rs")
+                rs[i] = rsp.tile([P, 8], F32, name="rs%d" % i, tag="rs")
                 nc.gpsimd.tensor_scalar(
                     out=ms[i][:, 0:5], in0=vv[i][:, 0:5], scalar1=1.0, scalar2=EPS, op0=ALU.mult, op1=ALU.add
                 )

@@ -295,17 +295,17 @@ def tile_glamemoryreader_pb_t_kernel(
             if s == 1:
                 prep_weight("o")
                 prep_vec()
-            op_b(s - 1)
-            op_j(s - 5)
             op_c(s - 3)
-            op_e(s - 4)
             op_t(s - 3)
-            op_f(s)
             op_mr(s)
+            op_b(s - 1)
+            op_e(s - 4)
             op_xv(s - 2)
-            op_d(s - 3)
-            op_pow(s - 1)
-            op_tq(s + 2)
-            op_k(s - 5)
             op_a(s + 1)
+            op_j(s - 5)
+            op_f(s)
+            op_tq(s + 2)
+            op_d(s - 3)
+            op_k(s - 5)
             op_mx(s - 4)
+            op_pow(s - 1)

@@ -22,6 +22,17 @@ EPS = 1e-5
 
 D_MOD = 5
 D_ON_ACT = (1, 3)
+D_LAST = NT - GT
+X = 1
+W_ON_S = (0, 2, 4, 6)
+
+LOADS = "lw:0 lq0:0 lh0:0 lv:0 lw:1 lh0:1 lw:2 lv:1 lw:3 ls:0 lq0:1 lw:4 lw:5 lw:6 lw:7 lh0:2 lh0:3 lq:1 lh:1 ls:1"
+PROLOGUE = (
+    "wt:0 tq:0 wt:1 wc:0 f:0 px:0 wc:1 a:0 wt:2 wt:3 pn:0 f:1 wq:0 wq:1 mr:0 tq:1 "
+    "wc:2 wc:3 b:0 xv:0 wt:4 wt:5 wq:2 wq:3 a:1 mr:1 mr:2 wc:4 wc:5 b:1 pow:0 wt:6 "
+    "wt:7 wq:4 wq:5 wc:6 wc:7 pv:0 tq:2 f:2 pow:1 wq:6 wq:7 t:-1 xv:1 d:-1 f:3 c:0 "
+    "b:2 t:0 e:-1 f:4 "
+)
 
 FLOPS = 2 * TOK * D * D * 2 + 2 * TOK * H * HK * HV
 
@@ -38,7 +49,7 @@ def tile_glamemoryreader_pb_t_kernel(
         const = ctx.enter_context(tc.tile_pool(name="const", bufs=1))
         io = ctx.enter_context(tc.tile_pool(name="io", bufs=4))
         ob = ctx.enter_context(tc.tile_pool(name="ob", bufs=3))
-        mid = ctx.enter_context(tc.tile_pool(name="mid", bufs=4))
+        mid = ctx.enter_context(tc.tile_pool(name="mid", bufs=8))
         qtp = ctx.enter_context(tc.tile_pool(name="qtp", bufs=3))
         cod = ctx.enter_context(tc.tile_pool(name="cod", bufs=4))
         stat = ctx.enter_context(tc.tile_pool(name="stat", bufs=8))
@@ -47,7 +58,7 @@ def tile_glamemoryreader_pb_t_kernel(
         psum_q = ctx.enter_context(tc.psum_pool(name="psumq", bufs=1))
         psum_r = ctx.enter_context(tc.psum_pool(name="psumr", bufs=3))
         psum_t = ctx.enter_context(tc.psum_pool(name="psumt", bufs=1))
-        psum_o = ctx.enter_context(tc.psum_pool(name="psumo", bufs=2))
+        psum_o = ctx.enter_context(tc.psum_pool(name="psumo", bufs=1))
         ctx.enter_context(tc.manual_schedule())
 
         wrow = const.tile([P, D + HV], BF16, name="wrow", tag="wrow")
@@ -101,48 +112,78 @@ def tile_glamemoryreader_pb_t_kernel(
         def grp(ap, g):
             return ap[g * GT * P : (g + 1) * GT * P, :].rearrange("(p j) d -> p j d", j=GT)
 
-        def load(g):
-            q_t[g] = io.tile([P, GT, D], BF16, name="q%d" % g, tag="q")
-            h_t[g] = io.tile([P, GT, D], BF16, name="h%d" % g, tag="h")
-            if g > 0:
-                nc.sync.dma_start(out=q_t[g][:], in_=grp(qs, g))
-                nc.sync.dma_start(out=h_t[g][:], in_=grp(hs, g))
-            else:
-                first, second = slice(0, 2), slice(2, 4)
-                states = recurrent_state.rearrange("b h k v -> k (b h) v")
-                nc.sync.dma_start(out=q_t[g][:, first, :], in_=grp(qs, g)[:, first, :])
-                nc.sync.dma_start(out=s_sb[:, 0:H, :], in_=states[:, 0:H, :])
-                nc.sync.dma_start(out=w_raw["g"][:], in_=gate_w.rearrange("(a p) k -> p a k", p=P))
-                nc.sync.dma_start(out=h_t[g][:, first, :], in_=grp(hs, g)[:, first, :])
-                nc.sync.dma_start(out=w_raw["o"][:], in_=o_w.rearrange("(a p) k -> p a k", p=P))
-                nc.sync.dma_start(out=wrow[0:1, 0:D], in_=norm_w.rearrange("(o c) -> o c", o=1))
-                nc.sync.dma_start(out=wrow[0:1, D : D + HV], in_=v_norm_w.rearrange("(o c) -> o c", o=1))
-                nc.sync.dma_start(out=q_t[g][:, second, :], in_=grp(qs, g)[:, second, :])
-                nc.sync.dma_start(out=h_t[g][:, second, :], in_=grp(hs, g)[:, second, :])
-                nc.sync.dma_start(out=s_sb[:, H:, :], in_=states[:, H:, :])
+        first, second = slice(0, 2), slice(2, 4)
+        states = recurrent_state.rearrange("b h k v -> k (b h) v")
 
-        def prep_vec():
+        def op_lq(g):
+            q_t[g] = io.tile([P, GT, D], BF16, name="q%d" % g, tag="q")
+            nc.sync.dma_start(out=q_t[g][:], in_=grp(qs, g))
+
+        def op_lh(g):
+            h_t[g] = io.tile([P, GT, D], BF16, name="h%d" % g, tag="h")
+            nc.sync.dma_start(out=h_t[g][:], in_=grp(hs, g))
+
+        def op_lq0(j):
+            if j == 0:
+                q_t[0] = io.tile([P, GT, D], BF16, name="q0", tag="q")
+            sl = slice(2 * j, 2 * j + 2)
+            nc.sync.dma_start(out=q_t[0][:, sl, :], in_=grp(qs, 0)[:, sl, :])
+
+        def op_lh0(j):
+            if j == 0:
+                h_t[0] = io.tile([P, GT, D], BF16, name="h0", tag="h")
+            nc.sync.dma_start(out=h_t[0][:, j, :], in_=grp(hs, 0)[:, j, :])
+
+        def op_ls(j):
+            sl = slice(0, H) if j == 0 else slice(H, B * H)
+            nc.sync.dma_start(out=s_sb[:, sl, :], in_=states[:, sl, :])
+
+        def op_lw(j):
+            nm, a = "go"[j // 4], j % 4
+            src = (gate_w if nm == "g" else o_w).rearrange("(a p) k -> p a k", p=P)
+            nc.sync.dma_start(out=w_raw[nm][:, a, :], in_=src[:, a, :])
+
+        def op_lv(j):
+            if j == 0:
+                nc.sync.dma_start(out=wrow[0:1, 0:D], in_=norm_w.rearrange("(o c) -> o c", o=1))
+            else:
+                nc.sync.dma_start(out=wrow[0:1, D : D + HV], in_=v_norm_w.rearrange("(o c) -> o c", o=1))
+
+        def op_pn(j):
             nc.tensor.matmul(out=nw_bc[:], lhsT=ones[:], rhs=wrow[:, 0:D], start=True, stop=True)
-            b_ps = psum_o.tile([P, D], F32, name="vw_ps", tag="O")
+
+        def op_pv(j):
+            b_ps = psum_o.tile([P, D], F32, name="vw_ps", tag="G")
             nc.tensor.matmul(out=b_ps[:, 0:HV], lhsT=ones[:], rhs=wrow[:, D : D + HV], start=True, stop=True)
             nc.vector.tensor_copy(out=vw_bc[:], in_=b_ps[:, 0:HV])
 
-        def prep_weight(nm):
-            words = w_raw[nm][:].bitcast(F32)
-            for half in range(2):
-                wps = psum_o.tile([P, 2, 2, P], F32, name="wps_%s%d" % (nm, half), tag="O")
-                for k in range(2):
-                    for u in range(2):
-                        nc.tensor.transpose(wps[:, k, u, :], words[:, half * 2 + k, u * P : (u + 1) * P], ident_f[:])
-                wg = const.tile([P, 1024], BF16, name="wg_%s%d" % (nm, half), tag="wg_%s%d" % (nm, half), align_bytes=64)
-                dst = wg[:].bitcast(F32).rearrange("p (a t u) -> p a t u", a=2, u=2)
-                nc.vector.tensor_copy(out=dst, in_=wps[:].rearrange("p a u t -> p a t u"))
-                sl = slice(half * 256, (half + 1) * 256)
-                nc.vector.quantize_mx(out=w_codes[nm][:, sl].bitcast(FP8X4), scales=w_scales[nm][:, sl], in_=wg[:])
+        wps = {}
+        wg = {}
 
-        def op_tq(i):
-            if ok(i) and i % 2 == 0:
-                u = i // 2
+        def op_wt(j):
+            nm, a = "go"[j // 4], j % 4
+            words = w_raw[nm][:, a, :].bitcast(F32)
+            wps[j] = psum_o.tile([P, 2, P], F32, name="wps%d" % j, tag="GP"[j % 2])
+            for u in range(2):
+                nc.tensor.transpose(wps[j][:, u, :], words[:, u * P : (u + 1) * P], ident_f[:])
+
+        def op_wc(j):
+            wg[j] = const.tile([P, 512], BF16, name="wg_%d" % j, tag="wg_%d" % j, align_bytes=64)
+            dst = wg[j][:].bitcast(F32).rearrange("p (t u) -> p t u", u=2)
+            src = wps[j][:].rearrange("p u t -> p t u")
+            if j in W_ON_S:
+                nc.scalar.copy(out=dst, in_=src)
+            else:
+                nc.vector.tensor_copy(out=dst, in_=src)
+
+        def op_wq(j):
+            nm, a = "go"[j // 4], j % 4
+            sl = slice(a * P, (a + 1) * P)
+            nc.vector.quantize_mx(out=w_codes[nm][:, sl].bitcast(FP8X4), scales=w_scales[nm][:, sl], in_=wg[j][:])
+
+        def op_tq(u):
+            i = 2 * u
+            if ok(i):
                 qTp[u] = psum_q.tile([P, 2, H, P], BF16, name="qTp%d" % u, tag="qTp")
                 for half in range(2):
                     for h in range(H):
@@ -152,9 +193,8 @@ def tile_glamemoryreader_pb_t_kernel(
                             ident_b[:],
                         )
 
-        def op_a(i):
-            if ok(i) and i % 2 == 0:
-                u = i // 2
+        def op_a(u):
+            if ok(2 * u):
                 qT[u] = qtp.tile([P, 2, H, P], BF16, name="qT%d" % u, tag="qT")
                 nc.scalar.copy(out=qT[u][:], in_=qTp[u][:])
 
@@ -171,15 +211,28 @@ def tile_glamemoryreader_pb_t_kernel(
                         stop=True,
                     )
 
+        vx = stat.tile([P, 8], F32, name="vx", tag="vx")
+        mx_ = stat.tile([P, 8], F32, name="mx_", tag="mx_")
+        rx = stat.tile([P, 8], F32, name="rx", tag="rx")
+
+        def stats(u):
+            if u not in vv:
+                vv[u] = stat.tile([P, 8], F32, name="vv%d" % (u + X), tag="vv")
+            return vv[u]
+
+        def op_px(j):
+            cols = slice(0, X)
+            nc.gpsimd.tensor_scalar(out=mx_[:, cols], in0=vx[:, cols], scalar1=1.0, scalar2=EPS, op0=ALU.mult, op1=ALU.add)
+            nc.gpsimd.tensor_tensor(out=rx[:, cols], in0=mx_[:, cols], in1=neghalf[:, cols], op=ALU.pow)
+
         def op_f(i):
             if ok(i):
-                vv[i] = stat.tile([P, 8], F32, name="vv%d" % i, tag="vv")
                 nc.scalar.activation(
                     out=junk_h[:],
                     in_=h_t[i // GT][:, i % GT, :],
                     func=ACTF.Square,
                     scale=1.0 / math.sqrt(D),
-                    accum_out=vv[i][:, 4:5],
+                    accum_out=(stats(i - X)[:, 4:5] if i >= X else vx[:, i : i + 1]),
                 )
 
         def op_b(i):
@@ -190,17 +243,18 @@ def tile_glamemoryreader_pb_t_kernel(
                         in_=r_ps[i][:, h * HV : (h + 1) * HV],
                         func=ACTF.Square,
                         scale=1.0 / math.sqrt(HV),
-                        accum_out=vv[i][:, h : h + 1],
+                        accum_out=stats(i)[:, h : h + 1],
                     )
 
-        def op_pow(i):
-            if ok(i):
-                ms[i] = stat.tile([P, 8], F32, name="ms%d" % i, tag="ms")
-                rs[i] = rsp.tile([P, 8], F32, name="rs%d" % i, tag="rs")
+        def op_pow(u):
+            if ok(u):
+                cols = slice(0, 5 if ok(u + X) else 4)
+                ms[u] = stat.tile([P, 8], F32, name="ms%d" % (u + X), tag="ms")
+                rs[u] = rsp.tile([P, 8], F32, name="rs%d" % (u + X), tag="rs")
                 nc.gpsimd.tensor_scalar(
-                    out=ms[i][:, 0:5], in0=vv[i][:, 0:5], scalar1=1.0, scalar2=EPS, op0=ALU.mult, op1=ALU.add
+                    out=ms[u][:, cols], in0=vv[u][:, cols], scalar1=1.0, scalar2=EPS, op0=ALU.mult, op1=ALU.add
                 )
-                nc.gpsimd.tensor_tensor(out=rs[i][:, 0:5], in0=ms[i][:, 0:5], in1=neghalf[:, 0:5], op=ALU.pow)
+                nc.gpsimd.tensor_tensor(out=rs[u][:, cols], in0=ms[u][:, cols], in1=neghalf[:, cols], op=ALU.pow)
 
         def op_xv(i):
             if ok(i):
@@ -208,7 +262,7 @@ def tile_glamemoryreader_pb_t_kernel(
                 nc.vector.scalar_tensor_tensor(
                     out=xb[i][:],
                     in0=h_t[i // GT][:, i % GT, :],
-                    scalar=rs[i][:, 4:5],
+                    scalar=(rs[i - X][:, 4:5] if i >= X else rx[:, i : i + 1]),
                     in1=nw_bc[:],
                     op0=ALU.mult,
                     op1=ALU.mult,
@@ -228,29 +282,35 @@ def tile_glamemoryreader_pb_t_kernel(
                         op1=ALU.mult,
                     )
 
+        def parts(i):
+            return ([0] if i + 1 < NT else []) + ([1] if ok(i) else [])
+
         def op_t(i):
-            if ok(i):
-                tp[i] = psum_t.tile([P, 2, 2, P], F32, name="tp%d" % i, tag="T")
-                for c, src in enumerate((xb[i], nb[i])):
-                    words = src[:].bitcast(F32)
+            if i >= -1 and parts(i):
+                tp[i] = psum_t.tile([P, 2, 2, P], F32, name="tp%d" % (i + 1), tag="T")
+                for c in parts(i):
+                    words = (nb[i] if c else xb[i + 1])[:].bitcast(F32)
                     for u in range(2):
                         nc.tensor.transpose(tp[i][:, c, u, :], words[:, u * P : (u + 1) * P], ident_f[:])
 
         def op_d(i):
-            if ok(i):
-                xng[i] = mid.tile([P, 1024], BF16, name="xng%d" % i, tag="xng", align_bytes=64)
-                dst = xng[i][:].bitcast(F32).rearrange("p (c t u) -> p c t u", c=2, u=2)
-                src = tp[i][:].rearrange("p c u t -> p c t u")
-                if i % D_MOD in D_ON_ACT:
+            if i >= -1 and parts(i):
+                lo, hi = parts(i)[0], parts(i)[-1] + 1
+                xng[i] = mid.tile([P, 1024], BF16, name="xng%d" % (i + 1), tag="xng", align_bytes=64)
+                dst = xng[i][:].bitcast(F32).rearrange("p (c t u) -> p c t u", c=2, u=2)[:, lo:hi]
+                src = tp[i][:].rearrange("p c u t -> p c t u")[:, lo:hi]
+                if i % D_MOD in D_ON_ACT or i >= D_LAST:
                     nc.scalar.copy(out=dst, in_=src)
                 else:
                     nc.vector.tensor_copy(out=dst, in_=src)
 
         def op_e(i):
-            if ok(i):
-                xnc[i] = cod.tile([P, 256], U32, name="xnc%d" % i, tag="xnc", align_bytes=64)
-                xns[i] = cod.tile([P, 256], U8, name="xns%d" % i, tag="xns", align_bytes=64)
-                nc.vector.quantize_mx(out=xnc[i][:].bitcast(FP8X4), scales=xns[i][:], in_=xng[i][:])
+            if i >= -1 and parts(i):
+                lo, hi = parts(i)[0], parts(i)[-1] + 1
+                xnc[i] = cod.tile([P, 256], U32, name="xnc%d" % (i + 1), tag="xnc", align_bytes=64)
+                xns[i] = cod.tile([P, 256], U8, name="xns%d" % (i + 1), tag="xns", align_bytes=64)
+                sl = slice(lo * P, hi * P)
+                nc.vector.quantize_mx(out=xnc[i][:, sl].bitcast(FP8X4), scales=xns[i][:, sl], in_=xng[i][:, lo * 512 : hi * 512])
 
         def mx(dst, i, c, nm):
             sl = slice(c * P, (c + 1) * P)
@@ -265,16 +325,17 @@ def tile_glamemoryreader_pb_t_kernel(
             )
 
         def op_mx(i):
-            if ok(i):
-                g_ps[i] = psum_o.tile([P, D], F32, name="g%d" % i, tag="O")
-                mx(g_ps[i], i, 0, "g")
-                p_ps[i] = psum_o.tile([P, D], F32, name="p%d" % i, tag="O")
+            if i >= -1 and 0 in parts(i):
+                g_ps[i + 1] = psum_o.tile([P, D], F32, name="g%d" % (i + 1), tag="G")
+                mx(g_ps[i + 1], i, 0, "g")
+            if 1 in parts(i):
+                p_ps[i] = psum_o.tile([P, D], F32, name="p%d" % i, tag="P")
                 mx(p_ps[i], i, 1, "o")
 
         def op_j(i):
-            if ok(i):
-                gate[i] = cod.tile([P, D], F32, name="gate%d" % i, tag="gate")
-                nc.scalar.activation(out=gate[i][:], in_=g_ps[i][:], func=ACTF.Sigmoid)
+            if ok(i + 1):
+                gate[i + 1] = cod.tile([P, D], F32, name="gate%d" % (i + 1), tag="gate")
+                nc.scalar.activation(out=gate[i + 1][:], in_=g_ps[i + 1][:], func=ACTF.Sigmoid)
 
         def op_k(i):
             if ok(i):
@@ -287,25 +348,34 @@ def tile_glamemoryreader_pb_t_kernel(
                 elif i % GT == GT - 1:
                     nc.sync.dma_start(out=grp(os_, g), in_=o_t[g][:])
 
-        for s in range(-10, NT + 6):
-            if (s + 10) % GT == 0 and (s + 10) // GT < NG:
-                load((s + 10) // GT)
-            if s == -1:
-                prep_weight("g")
-            if s == 1:
-                prep_weight("o")
-                prep_vec()
-            op_c(s - 3)
-            op_t(s - 3)
-            op_mr(s)
-            op_b(s - 1)
-            op_e(s - 4)
-            op_xv(s - 2)
-            op_a(s + 1)
-            op_j(s - 5)
-            op_f(s)
-            op_tq(s + 2)
-            op_d(s - 3)
-            op_k(s - 5)
-            op_mx(s - 4)
-            op_pow(s - 1)
+        ops = dict(px=op_px, lq=op_lq, lh=op_lh, lq0=op_lq0, lh0=op_lh0, ls=op_ls, lw=op_lw, lv=op_lv, pn=op_pn, pv=op_pv, wt=op_wt, wc=op_wc, wq=op_wq,
+                   tq=op_tq, a=op_a, mr=op_mr, f=op_f, b=op_b, pow=op_pow, xv=op_xv, c=op_c, t=op_t, d=op_d, e=op_e, mx=op_mx, j=op_j, k=op_k)
+        done = set()
+
+        def once(nm, i):
+            if (nm, i) not in done:
+                done.add((nm, i))
+                ops[nm](i)
+
+        for word in (LOADS + " " + PROLOGUE).split():
+            nm, i = word.split(":")
+            once(nm, int(i))
+
+        for s in range(-3, NT + 6):
+            once("t", s - 3)
+            once("b", s - 1)
+            once("pow", s - 1)
+            once("a", (s + 1) // 2)
+            once("mr", s)
+            once("j", s - 5)
+            once("k", s - 5)
+            once("tq", (s + 3) // 2)
+            once("f", s + X)
+            once("d", s - 3)
+            once("c", s - 2)
+            once("e", s - 3)
+            once("mx", s - 4)
+            once("xv", s - 1 + X)
+            if (s + 10) % GT == 0 and 0 < (s + 10) // GT < NG:
+                once("lq", (s + 10) // GT)
+                once("lh", (s + 10) // GT)

@@ -329,7 +329,10 @@ def tile_glamemoryreader_pb_t_kernel(
                 g_ps[i + 1] = psum_o.tile([P, D], F32, name="g%d" % (i + 1), tag="G")
                 mx(g_ps[i + 1], i, 0, "g")
             if 1 in parts(i):
-                p_ps[i] = psum_o.tile([P, D], F32, name="p%d" % i, tag="P")
+                if i < NT - 1:
+                    p_ps[i] = psum_o.tile([P, D], F32, name="p%d" % i, tag="P")
+                else:
+                    p_ps[i] = psum_r.tile([P, D], F32, name="p%d" % i, tag="r")
                 mx(p_ps[i], i, 1, "o")
 
         def op_j(i):
@@ -342,10 +345,12 @@ def tile_glamemoryreader_pb_t_kernel(
                 g = i // GT
                 if i % GT == 0:
                     o_t[g] = ob.tile([P, GT, D], F32, name="o%d" % g, tag="o")
-                nc.vector.tensor_tensor(out=o_t[g][:, i % GT, :], in0=p_ps[i][:], in1=gate[i][:], op=ALU.mult)
-                if g == NG - 1:
-                    nc.sync.dma_start(out=grp(os_, g)[:, i % GT, :], in_=o_t[g][:, i % GT, :])
-                elif i % GT == GT - 1:
+                cols = [slice(0, D)] if i < NT - 1 else [slice(0, D // 2), slice(D // 2, D)]
+                for sl in cols:
+                    nc.vector.tensor_tensor(out=o_t[g][:, i % GT, sl], in0=p_ps[i][:, sl], in1=gate[i][:, sl], op=ALU.mult)
+                    if g == NG - 1:
+                        nc.sync.dma_start(out=grp(os_, g)[:, i % GT, sl], in_=o_t[g][:, i % GT, sl])
+                if g < NG - 1 and i % GT == GT - 1:
                     nc.sync.dma_start(out=grp(os_, g), in_=o_t[g][:])
 
         ops = dict(px=op_px, lq=op_lq, lh=op_lh, lq0=op_lq0, lh0=op_lh0, ls=op_ls, lw=op_lw, lv=op_lv, pn=op_pn, pv=op_pv, wt=op_wt, wc=op_wc, wq=op_wq,

from contextlib import ExitStack
import math

import concourse.mybir as mybir
from concourse.masks import make_identity

F32 = mybir.dt.float32
BF16 = mybir.dt.bfloat16
U32 = mybir.dt.uint32
U8 = mybir.dt.uint8
FP8X4 = mybir.dt.float8_e4m3fn_x4
ACTF = mybir.ActivationFunctionType
ALU = mybir.AluOpType

P = 128
B, T, D, H, HK, HV = 4, 2048, 512, 4, 128, 128
TOK = B * T
NT = TOK // P
GT = 4
NG = NT // GT
EPS = 1e-5

D_MOD = 5
D_ON_ACT = (1, 3)
D_LAST = NT - GT
X = 1
W_ON_S = (0, 2, 4, 6)

LOADS = "lw:0 lq0:0 lh0:0 lv:0 lw:1 lh0:1 lw:2 lv:1 lw:3 ls:0 lq0:1 lw:4 lw:5 lw:6 lw:7 lh0:2 lh0:3 lq:1 lh:1 ls:1"
PROLOGUE = (
    "wt:0 tq:0 wt:1 wc:0 f:0 px:0 wc:1 a:0 wt:2 wt:3 pn:0 f:1 wq:0 wq:1 mr:0 tq:1 "
    "wc:2 wc:3 b:0 xv:0 wt:4 wt:5 wq:2 wq:3 a:1 mr:1 mr:2 wc:4 wc:5 b:1 pow:0 wt:6 "
    "wt:7 wq:4 wq:5 wc:6 wc:7 pv:0 tq:2 f:2 pow:1 wq:6 wq:7 t:-1 xv:1 d:-1 f:3 c:0 "
    "b:2 t:0 e:-1 f:4 "
)

FLOPS = 2 * TOK * D * D * 2 + 2 * TOK * H * HK * HV


def tile_glamemoryreader_pb_t_kernel(
    tc, hidden_states, norm_w, gate_w, q_hat, recurrent_state, v_norm_w, o_w, out
):
    nc = tc.nc
    hs = hidden_states.rearrange("b t d -> (b t) d")
    qs = q_hat.rearrange("b t h k -> (b t) (h k)")
    os_ = out.rearrange("b t d -> (b t) d")

    with ExitStack() as ctx:
        const = ctx.enter_context(tc.tile_pool(name="const", bufs=1))
        io = ctx.enter_context(tc.tile_pool(name="io", bufs=4))
        ob = ctx.enter_context(tc.tile_pool(name="ob", bufs=3))
        mid = ctx.enter_context(tc.tile_pool(name="mid", bufs=8))
        qtp = ctx.enter_context(tc.tile_pool(name="qtp", bufs=3))
        cod = ctx.enter_context(tc.tile_pool(name="cod", bufs=4))
        stat = ctx.enter_context(tc.tile_pool(name="stat", bufs=8))
        rsp = ctx.enter_context(tc.tile_pool(name="rsp", bufs=2))
        psum_w = ctx.enter_context(tc.psum_pool(name="psumw", bufs=1))
        psum_q = ctx.enter_context(tc.psum_pool(name="psumq", bufs=1))
        psum_r = ctx.enter_context(tc.psum_pool(name="psumr", bufs=3))
        psum_t = ctx.enter_context(tc.psum_pool(name="psumt", bufs=1))
        psum_o = ctx.enter_context(tc.psum_pool(name="psumo", bufs=1))
        ctx.enter_context(tc.manual_schedule())

        wrow = const.tile([P, D + HV], BF16, name="wrow", tag="wrow")
        ones = const.tile([P, P], BF16, name="ones", tag="ones")
        nw_bc = psum_w.tile([P, D], F32, name="nw_bc", tag="nw_bc")
        vw_bc = const.tile([P, HV], BF16, name="vw_bc", tag="vw_bc")
        ident_b = const.tile([P, P], BF16, name="ident_b", tag="ident_b")
        ident_f = const.tile([P, P], F32, name="ident_f", tag="ident_f")
        neghalf = const.tile([P, 8], F32, name="neghalf", tag="neghalf")
        scr = const.tile([P, 1], F32, name="scr", tag="scr")
        junk_h = const.tile([P, D], BF16, name="junk_h", tag="junk_h")
        junk_r = const.tile([P, D], BF16, name="junk_r", tag="junk_r")
        s_sb = const.tile([P, B * H, HV], BF16, name="s_sb", tag="s_sb")
        w_raw = {}
        w_codes = {}
        w_scales = {}
        for nm in ("g", "o"):
            w_raw[nm] = const.tile([P, 4, D], BF16, name="wraw_" + nm, tag="wraw_" + nm)
            w_codes[nm] = const.tile([P, D], U32, name="wc_" + nm, tag="wc_" + nm, align_bytes=64)
            w_scales[nm] = const.tile([P, D], U8, name="ws_" + nm, tag="ws_" + nm, align_bytes=64)

        nc.vector.memset(wrow[:], 0.0)
        nc.vector.memset(ones[:], 1.0)
        nc.vector.memset(neghalf[:], -0.5)
        nc.scalar.activation(out=scr[:], in_=neghalf[:, 0:1], func=ACTF.Sigmoid)
        make_identity(nc, ident_b[:])
        make_identity(nc, ident_f[:])

        h_t = {}
        q_t = {}
        o_t = {}
        qTp = {}
        qT = {}
        r_ps = {}
        ms = {}
        vv = {}
        rs = {}
        xb = {}
        nb = {}
        tp = {}
        xng = {}
        xnc = {}
        xns = {}
        g_ps = {}
        p_ps = {}
        gate = {}

        def ok(i):
            return 0 <= i < NT

        def grp(ap, g):
            return ap[g * GT * P : (g + 1) * GT * P, :].rearrange("(p j) d -> p j d", j=GT)

        first, second = slice(0, 2), slice(2, 4)
        states = recurrent_state.rearrange("b h k v -> k (b h) v")

        def op_lq(g):
            q_t[g] = io.tile([P, GT, D], BF16, name="q%d" % g, tag="q")
            nc.sync.dma_start(out=q_t[g][:], in_=grp(qs, g))

        def op_lh(g):
            h_t[g] = io.tile([P, GT, D], BF16, name="h%d" % g, tag="h")
            nc.sync.dma_start(out=h_t[g][:], in_=grp(hs, g))

        def op_lq0(j):
            if j == 0:
                q_t[0] = io.tile([P, GT, D], BF16, name="q0", tag="q")
            sl = slice(2 * j, 2 * j + 2)
            nc.sync.dma_start(out=q_t[0][:, sl, :], in_=grp(qs, 0)[:, sl, :])

        def op_lh0(j):
            if j == 0:
                h_t[0] = io.tile([P, GT, D], BF16, name="h0", tag="h")
            nc.sync.dma_start(out=h_t[0][:, j, :], in_=grp(hs, 0)[:, j, :])

        def op_ls(j):
            sl = slice(0, H) if j == 0 else slice(H, B * H)
            nc.sync.dma_start(out=s_sb[:, sl, :], in_=states[:, sl, :])

        def op_lw(j):
            nm, a = "go"[j // 4], j % 4
            src = (gate_w if nm == "g" else o_w).rearrange("(a p) k -> p a k", p=P)
            nc.sync.dma_start(out=w_raw[nm][:, a, :], in_=src[:, a, :])

        def op_lv(j):
            if j == 0:
                nc.sync.dma_start(out=wrow[0:1, 0:D], in_=norm_w.rearrange("(o c) -> o c", o=1))
            else:
                nc.sync.dma_start(out=wrow[0:1, D : D + HV], in_=v_norm_w.rearrange("(o c) -> o c", o=1))

        def op_pn(j):
            nc.tensor.matmul(out=nw_bc[:], lhsT=ones[:], rhs=wrow[:, 0:D], start=True, stop=True)

        def op_pv(j):
            b_ps = psum_o.tile([P, D], F32, name="vw_ps", tag="G")
            nc.tensor.matmul(out=b_ps[:, 0:HV], lhsT=ones[:], rhs=wrow[:, D : D + HV], start=True, stop=True)
            nc.vector.tensor_copy(out=vw_bc[:], in_=b_ps[:, 0:HV])

        wps = {}
        wg = {}

        def op_wt(j):
            nm, a = "go"[j // 4], j % 4
            words = w_raw[nm][:, a, :].bitcast(F32)
            wps[j] = psum_o.tile([P, 2, P], F32, name="wps%d" % j, tag="GP"[j % 2])
            for u in range(2):
                nc.tensor.transpose(wps[j][:, u, :], words[:, u * P : (u + 1) * P], ident_f[:])

        def op_wc(j):
            wg[j] = const.tile([P, 512], BF16, name="wg_%d" % j, tag="wg_%d" % j, align_bytes=64)
            dst = wg[j][:].bitcast(F32).rearrange("p (t u) -> p t u", u=2)
            src = wps[j][:].rearrange("p u t -> p t u")
            if j in W_ON_S:
                nc.scalar.copy(out=dst, in_=src)
            else:
                nc.vector.tensor_copy(out=dst, in_=src)

        def op_wq(j):
            nm, a = "go"[j // 4], j % 4
            sl = slice(a * P, (a + 1) * P)
            nc.vector.quantize_mx(out=w_codes[nm][:, sl].bitcast(FP8X4), scales=w_scales[nm][:, sl], in_=wg[j][:])

        def op_tq(u):
            i = 2 * u
            if ok(i):
                qTp[u] = psum_q.tile([P, 2, H, P], BF16, name="qTp%d" % u, tag="qTp")
                for half in range(2):
                    for h in range(H):
                        nc.tensor.transpose(
                            qTp[u][:, half, h, :],
                            q_t[i // GT][:, i % GT + half, h * HK : (h + 1) * HK],
                            ident_b[:],
                        )

        def op_a(u):
            if ok(2 * u):
                qT[u] = qtp.tile([P, 2, H, P], BF16, name="qT%d" % u, tag="qT")
                nc.scalar.copy(out=qT[u][:], in_=qTp[u][:])

        def op_mr(i):
            if ok(i):
                b = i // (NT // B)
                r_ps[i] = psum_r.tile([P, D], F32, name="r%d" % i, tag="r")
                for h in range(H):
                    nc.tensor.matmul(
                        out=r_ps[i][:, h * HV : (h + 1) * HV],
                        lhsT=qT[i // 2][:, i % 2, h, :],
                        rhs=s_sb[:, b * H + h, :],
                        start=True,
                        stop=True,
                    )

        vx = stat.tile([P, 8], F32, name="vx", tag="vx")
        mx_ = stat.tile([P, 8], F32, name="mx_", tag="mx_")
        rx = stat.tile([P, 8], F32, name="rx", tag="rx")

        def stats(u):
            if u not in vv:
                vv[u] = stat.tile([P, 8], F32, name="vv%d" % (u + X), tag="vv")
            return vv[u]

        def op_px(j):
            cols = slice(0, X)
            nc.gpsimd.tensor_scalar(out=mx_[:, cols], in0=vx[:, cols], scalar1=1.0, scalar2=EPS, op0=ALU.mult, op1=ALU.add)
            nc.gpsimd.tensor_tensor(out=rx[:, cols], in0=mx_[:, cols], in1=neghalf[:, cols], op=ALU.pow)

        def op_f(i):
            if ok(i):
                nc.scalar.activation(
                    out=junk_h[:],
                    in_=h_t[i // GT][:, i % GT, :],
                    func=ACTF.Square,
                    scale=1.0 / math.sqrt(D),
                    accum_out=(stats(i - X)[:, 4:5] if i >= X else vx[:, i : i + 1]),
                )

        def op_b(i):
            if ok(i):
                for h in range(H):
                    nc.scalar.activation(
                        out=junk_r[:, h * HV : (h + 1) * HV],
                        in_=r_ps[i][:, h * HV : (h + 1) * HV],
                        func=ACTF.Square,
                        scale=1.0 / math.sqrt(HV),
                        accum_out=stats(i)[:, h : h + 1],
                    )

        def op_pow(u):
            if ok(u):
                cols = slice(0, 5 if ok(u + X) else 4)
                ms[u] = stat.tile([P, 8], F32, name="ms%d" % (u + X), tag="ms")
                rs[u] = rsp.tile([P, 8], F32, name="rs%d" % (u + X), tag="rs")
                nc.gpsimd.tensor_scalar(
                    out=ms[u][:, cols], in0=vv[u][:, cols], scalar1=1.0, scalar2=EPS, op0=ALU.mult, op1=ALU.add
                )
                nc.gpsimd.tensor_tensor(out=rs[u][:, cols], in0=ms[u][:, cols], in1=neghalf[:, cols], op=ALU.pow)

        def op_xv(i):
            if ok(i):
                xb[i] = mid.tile([P, D], BF16, name="xb%d" % i, tag="xb")
                nc.vector.scalar_tensor_tensor(
                    out=xb[i][:],
                    in0=h_t[i // GT][:, i % GT, :],
                    scalar=(rs[i - X][:, 4:5] if i >= X else rx[:, i : i + 1]),
                    in1=nw_bc[:],
                    op0=ALU.mult,
                    op1=ALU.mult,
                )

        def op_c(i):
            if ok(i):
                nb[i] = mid.tile([P, D], BF16, name="nb%d" % i, tag="nb")
                for h in range(H):
                    sl = slice(h * HV, (h + 1) * HV)
                    nc.vector.scalar_tensor_tensor(
                        out=nb[i][:, sl],
                        in0=r_ps[i][:, sl],
                        scalar=rs[i][:, h : h + 1],
                        in1=vw_bc[:],
                        op0=ALU.mult,
                        op1=ALU.mult,
                    )

        def parts(i):
            return ([0] if i + 1 < NT else []) + ([1] if ok(i) else [])

        def op_t(i):
            if i >= -1 and parts(i):
                tp[i] = psum_t.tile([P, 2, 2, P], F32, name="tp%d" % (i + 1), tag="T")
                for c in parts(i):
                    words = (nb[i] if c else xb[i + 1])[:].bitcast(F32)
                    for u in range(2):
                        nc.tensor.transpose(tp[i][:, c, u, :], words[:, u * P : (u + 1) * P], ident_f[:])

        def op_d(i):
            if i >= -1 and parts(i):
                lo, hi = parts(i)[0], parts(i)[-1] + 1
                xng[i] = mid.tile([P, 1024], BF16, name="xng%d" % (i + 1), tag="xng", align_bytes=64)
                dst = xng[i][:].bitcast(F32).rearrange("p (c t u) -> p c t u", c=2, u=2)[:, lo:hi]
                src = tp[i][:].rearrange("p c u t -> p c t u")[:, lo:hi]
                if i % D_MOD in D_ON_ACT or i >= D_LAST:
                    nc.scalar.copy(out=dst, in_=src)
                else:
                    nc.vector.tensor_copy(out=dst, in_=src)

        def op_e(i):
            if i >= -1 and parts(i):
                lo, hi = parts(i)[0], parts(i)[-1] + 1
                xnc[i] = cod.tile([P, 256], U32, name="xnc%d" % (i + 1), tag="xnc", align_bytes=64)
                xns[i] = cod.tile([P, 256], U8, name="xns%d" % (i + 1), tag="xns", align_bytes=64)
                sl = slice(lo * P, hi * P)
                nc.vector.quantize_mx(out=xnc[i][:, sl].bitcast(FP8X4), scales=xns[i][:, sl], in_=xng[i][:, lo * 512 : hi * 512])

        def mx(dst, i, c, nm):
            sl = slice(c * P, (c + 1) * P)
            nc.tensor.matmul_mx(
                out=dst[:],
                lhsT=xnc[i][:, sl].bitcast(FP8X4),
                lhsT_scale=xns[i][:, sl],
                rhs=w_codes[nm][:].bitcast(FP8X4),
                rhs_scale=w_scales[nm][:],
                start=True,
                stop=True,
            )

        def op_mx(i):
            if i >= -1 and 0 in parts(i):
                g_ps[i + 1] = psum_o.tile([P, D], F32, name="g%d" % (i + 1), tag="G")
                mx(g_ps[i + 1], i, 0, "g")
            if 1 in parts(i):
                if i < NT - 1:
                    p_ps[i] = psum_o.tile([P, D], F32, name="p%d" % i, tag="P")
                else:
                    p_ps[i] = psum_r.tile([P, D], F32, name="p%d" % i, tag="r")
                mx(p_ps[i], i, 1, "o")

        def op_j(i):
            if ok(i + 1):
                gate[i + 1] = cod.tile([P, D], F32, name="gate%d" % (i + 1), tag="gate")
                nc.scalar.activation(out=gate[i + 1][:], in_=g_ps[i + 1][:], func=ACTF.Sigmoid)

        def op_k(i):
            if ok(i):
                g = i // GT
                if i % GT == 0:
                    o_t[g] = ob.tile([P, GT, D], F32, name="o%d" % g, tag="o")
                cols = [slice(0, D)] if i < NT - 1 else [slice(0, D // 2), slice(D // 2, D)]
                for sl in cols:
                    nc.vector.tensor_tensor(out=o_t[g][:, i % GT, sl], in0=p_ps[i][:, sl], in1=gate[i][:, sl], op=ALU.mult)
                    if g == NG - 1:
                        nc.sync.dma_start(out=grp(os_, g)[:, i % GT, sl], in_=o_t[g][:, i % GT, sl])
                if g < NG - 1 and i % GT == GT - 1:
                    nc.sync.dma_start(out=grp(os_, g), in_=o_t[g][:])

        ops = dict(px=op_px, lq=op_lq, lh=op_lh, lq0=op_lq0, lh0=op_lh0, ls=op_ls, lw=op_lw, lv=op_lv, pn=op_pn, pv=op_pv, wt=op_wt, wc=op_wc, wq=op_wq,
                   tq=op_tq, a=op_a, mr=op_mr, f=op_f, b=op_b, pow=op_pow, xv=op_xv, c=op_c, t=op_t, d=op_d, e=op_e, mx=op_mx, j=op_j, k=op_k)
        done = set()

        def once(nm, i):
            if (nm, i) not in done:
                done.add((nm, i))
                ops[nm](i)

        for word in (LOADS + " " + PROLOGUE).split():
            nm, i = word.split(":")
            once(nm, int(i))

        for s in range(-3, NT + 6):
            once("t", s - 3)
            once("b", s - 1)
            once("pow", s - 1)
            once("a", (s + 1) // 2)
            once("mr", s)
            once("j", s - 5)
            once("k", s - 5)
            once("tq", (s + 3) // 2)
            once("f", s + X)
            once("d", s - 3)
            once("c", s - 2)
            once("e", s - 3)
            once("mx", s - 4)
            once("xv", s - 1 + X)
            if (s + 10) % GT == 0 and 0 < (s + 10) // GT < NG:
                once("lq", (s + 10) // GT)
                once("lh", (s + 10) // GT)
